import numpy as np
import ml_dtypes


def mxq(x, axis, fmt="e4m3"):
    dtype, down = {"e4m3": (ml_dtypes.float8_e4m3fn, 7), "e5m2": (ml_dtypes.float8_e5m2, 14)}[fmt]
    v = np.moveaxis(np.asarray(x, np.float32).astype(ml_dtypes.bfloat16).astype(np.float64), axis, -1)
    blocks = v.reshape(v.shape[:-1] + (-1, 32))
    amax = np.abs(blocks).max(-1, keepdims=True)
    byte = np.maximum(np.where(amax > 0, np.frexp(amax)[1] - 1 + 127, 0) - down, 1)
    scale = np.exp2(byte - 127.0)
    codes = (blocks / scale).astype(np.float32).astype(dtype).astype(np.float64)
    return np.moveaxis((codes * scale).reshape(v.shape), -1, axis)


WIDE = False


def mx_kscale(k):
    if not WIDE:
        return np.ones(k)
    levels = np.array([10, -10, 5, -5, 0])
    a = np.random.permutation(np.resize(levels, k // 512 * 4)).reshape(k // 512, 4)
    idx = np.arange(k)
    return np.exp2(a[idx // 512, idx % 128 // 32])


BF16 = ml_dtypes.bfloat16


def bf(x):
    return np.asarray(x, np.float32).astype(BF16)


def f64(x):
    return np.asarray(x).astype(np.float64)


B, D, C, SHOT, U, R = 2048, 1536, 128, 16, 4096, 8


def setup_inputs():
    s = mx_kscale(U)
    g = np.exp2(np.round(np.log2(s.mean())))
    basis = np.random.standard_normal((R, D)) * 1.5 / np.sqrt(R * D)
    zq = np.random.standard_normal((B, R))
    zc = np.random.standard_normal((C, R))
    zu = np.random.standard_normal((U, R))
    x1 = zq @ basis + np.random.standard_normal((B, D)) / np.sqrt(D)
    x2 = (zc @ basis)[:, None, :] + np.random.standard_normal((C, SHOT, D)) / np.sqrt(D)
    x3 = zu @ basis + np.random.standard_normal((U, D)) / np.sqrt(D)
    lg = -0.5 * ((zu[:, None, :] - zc[None, :, :]) ** 2).sum(-1)
    w = np.exp(lg - lg.max(1, keepdims=True))
    w = w / w.sum(1, keepdims=True)
    return {"x1": bf(x1.reshape(B, D, 1, 1)), "x2": bf(x2), "x3": bf(x3 * (g / s)[:, None]), "w": bf(w * (s / g)[:, None])}


def reference(x1, x2, x3, w):
    x1, x2, x3, w = f64(x1), f64(x2), f64(x3), f64(w)
    b = x1.shape[0]
    q = x1.reshape(b, -1)
    n_class, shot, d = x2.shape
    weighted_unlab = mxq(w, 0, "e4m3").T @ mxq(x3, 0, "e4m3")
    denom = shot + np.sum(w, axis=0)
    proto = (np.sum(x2, axis=1) + weighted_unlab) / denom[:, None]
    q2 = np.sum(q * q, axis=-1)
    p2 = np.sum(proto * proto, axis=-1)
    cross = mxq(q, 1, "e4m3") @ mxq(proto, 1, "e4m3").T
    return -(q2[:, None] + p2[None, :] - 2.0 * cross)

@@ -1,0 +1,266 @@
+from contextlib import ExitStack
+
+import concourse.bass as bass
+import concourse.mybir as mybir
+import concourse.tile as tile
+from concourse.masks import make_identity
+
+F32 = mybir.dt.float32
+BF16 = mybir.dt.bfloat16
+U32 = mybir.dt.uint32
+U8 = mybir.dt.uint8
+FP8X4 = mybir.dt.float8_e4m3fn_x4
+ALU = mybir.AluOpType
+ACT = mybir.ActivationFunctionType
+AX = mybir.AxisListType
+
+P = 128
+B, D, C, SHOT, U = 2048, 1536, 128, 16, 4096
+FLOPS = 2 * U * C * D + 2 * B * C * D
+
+S_COLS = 192
+
+
+def tile_proto_metric_semi_kernel(tc, x1, x2, x3, w, out):
+    nc = tc.nc
+    q_dram = x1.rearrange("(p t) d a b -> p t (d a b)", t=16)
+    x3_dram = x3.rearrange("(c p j) d -> c p j d", p=P, j=4)
+    x2_dram = x2.flatten_outer_dims().rearrange("(h p s) d -> h p s d", p=P, s=4)
+    w_dram = w.rearrange("(c p j) m -> p c j m", p=P, j=4)
+    out_dram = out.rearrange("(p t) j -> p t j", t=16)
+
+    with ExitStack() as ctx:
+        const = ctx.enter_context(tc.tile_pool(name="const", bufs=1))
+        keep = ctx.enter_context(tc.tile_pool(name="keep", bufs=1))
+        stream = ctx.enter_context(tc.tile_pool(name="stream", bufs=2))
+        psum = ctx.enter_context(tc.psum_pool(name="psum", bufs=1))
+
+        ident = const.tile([P, P], F32, name="ident")
+        make_identity(nc, ident)
+        sel_f = const.tile([P, 32], F32, name="sel_f")
+        nc.vector.tensor_reduce(out=sel_f, in_=ident.rearrange("p (n i) -> p n i", i=4), axis=AX.X, op=ALU.add)
+        sel = const.tile([P, 32], BF16, name="sel")
+        nc.vector.tensor_copy(out=sel, in_=sel_f)
+        ones = const.tile([P, 2], BF16, name="ones")
+        nc.vector.memset(ones, 1.0)
+
+        q_codes = keep.tile([P, 3, B], U32, name="q_codes", align_bytes=64)
+        q_scales = keep.tile([P, 3, B], U8, name="q_scales", align_bytes=64)
+        q2 = keep.tile([P, 16], F32, name="q2")
+        junk = keep.tile([P, D], BF16, name="junk")
+        o_sb = keep.tile([P, 16, C], F32, name="o_sb")
+        w_codes = keep.tile([P, 8 * C], U32, name="w_codes", align_bytes=64)
+        w_scales = keep.tile([P, 8 * C], U8, name="w_scales", align_bytes=64)
+
+        items = ["W0", "X0", "Q0", "X1", "Q1", "X2", "Z0", "Q2", "X3", "Z1", "Q3", "X4", "Z2", "Q4",
+                 "X5", "Z3", "Q5", "X6", "X7", "Q6", "Q7"]
+        depth = {"W": 1, "X": 3, "Q": 5, "Z": 2}
+        held = {"W": 0, "X": 0, "Q": 0, "Z": 0}
+        raw = {}
+        state = {"next": 0}
+
+        def load_ahead():
+            while state["next"] < len(items):
+                it = items[state["next"]]
+                kind, idx = it[0], int(it[1:])
+                if held[kind] >= depth[kind]:
+                    break
+                if kind == "W":
+                    t = keep.tile([P, 8, 4, C], BF16, name="w_sb", tag="big0")
+                    nc.sync.dma_start(out=t, in_=w_dram)
+                elif kind == "X":
+                    t = stream.tile([P, 4, D], BF16, name="x3raw", tag="x3raw", bufs=3)
+                    nc.sync.dma_start(out=t, in_=x3_dram[idx])
+                elif kind == "Z":
+                    t = stream.tile([P, 4, D], BF16, name="x2raw", tag="x2raw", bufs=2)
+                    nc.sync.dma_start(out=t, in_=x2_dram[idx])
+                else:
+                    t = stream.tile([P, 2 * D], BF16, name="qraw", tag="qraw", bufs=5)
+                    nc.sync.dma_start(out=t.rearrange("p (t d) -> p t d", t=2), in_=q_dram[:, 2 * idx:2 * idx + 2, :])
+                raw[it] = t
+                held[kind] += 1
+                state["next"] += 1
+
+        small = {}
+        wu = []
+        st = []
+
+        def do_w(w_sb):
+            w_g = keep.tile([P, 8, C, 4], BF16, name="w_g", tag="big1", align_bytes=64)
+            for h in range(2):
+                nc.vector.tensor_copy(out=w_g[:, 4 * h:4 * h + 4], in_=w_sb[:, 4 * h:4 * h + 4].rearrange("p c j m -> p c m j"))
+            for h in range(2):
+                nc.vector.quantize_mx(
+                    out=w_codes[:, 512 * h:512 * h + 512].bitcast(FP8X4),
+                    scales=w_scales[:, 512 * h:512 * h + 512],
+                    in_=w_g[:, 4 * h:4 * h + 4].rearrange("p c m j -> p (c m j)"),
+                )
+            den_ps = psum.tile([P, 2], F32, name="den_ps", tag="b0")
+            for c in range(8):
+                for j in range(4):
+                    nc.tensor.matmul(out=den_ps, lhsT=w_sb[:, c, j, :], rhs=ones,
+                                     start=(c == 0 and j == 0), stop=(c == 7 and j == 3))
+            den = const.tile([P, 1], F32, name="den")
+            nc.vector.tensor_scalar_add(out=den, in0=den_ps[:, 0:1], scalar1=float(SHOT))
+            rden = const.tile([P, 1], F32, name="rden")
+            nc.vector.reciprocal(out=rden, in_=den)
+            small["rden"] = rden
+
+        def regroup(copy, dst, src, lo, hi):
+            copy(out=dst[:, lo:hi, :].rearrange("p (c i) t -> p c t i", i=4),
+                 in_=src[:, :, lo:hi].rearrange("p t (c i) -> p c t i", i=4))
+
+        def do_x3(c, x_sb):
+            if c == 0:
+                for n in range(3):
+                    wu.append(psum.tile([P, 512], F32, name="wu%d" % n, tag="a%d" % n))
+            g = stream.tile([P, D, 4], BF16, name="x3g", tag="x3g", bufs=2, align_bytes=64)
+            codes = stream.tile([P, D], U32, name="x3c", tag="x3c", bufs=2, align_bytes=64)
+            scales = stream.tile([P, D], U8, name="x3s", tag="x3s", bufs=2, align_bytes=64)
+            regroup(nc.scalar.copy, g, x_sb, D - S_COLS, D)
+            regroup(nc.vector.tensor_copy, g, x_sb, 0, 512)
+            regroup(nc.vector.tensor_copy, g, x_sb, 512, 1024)
+            regroup(nc.vector.tensor_copy, g, x_sb, 1024, D - S_COLS)
+            for n in range(3):
+                cols = slice(512 * n, 512 * n + 512)
+                nc.vector.quantize_mx(out=codes[:, cols].bitcast(FP8X4), scales=scales[:, cols],
+                                      in_=g[:, cols, :].rearrange("p c t -> p (c t)"))
+            for n in range(3):
+                cols = slice(512 * n, 512 * n + 512)
+                nc.tensor.matmul_mx(out=wu[n], lhsT=w_codes[:, C * c:C * c + C].bitcast(FP8X4),
+                                    lhsT_scale=w_scales[:, C * c:C * c + C],
+                                    rhs=codes[:, cols].bitcast(FP8X4), rhs_scale=scales[:, cols],
+                                    start=(c == 0), stop=(c == 7))
+
+        def do_x2(h, z_sb):
+            if h == 0:
+                for b in range(3):
+                    st.append(psum.tile([P, 4, C], F32, name="st%d" % b, tag="b%d" % b))
+            for dt in range(12):
+                for s in range(4):
+                    nc.tensor.matmul(out=st[dt // 4][:, dt % 4, 32 * h:32 * h + 32],
+                                     lhsT=z_sb[:, s, P * dt:P * dt + P], rhs=sel,
+                                     start=(s == 0), stop=(s == 3))
+
+        def finish_x2():
+            st_sb = keep.tile([P, 12, C], F32, name="st_sb", tag="big0")
+            for b in range(3):
+                cp = nc.vector.tensor_copy if b == 1 else nc.scalar.copy
+                cp(out=st_sb[:, 4 * b:4 * b + 4, :], in_=st[b])
+            ssc = keep.tile([P, D], F32, name="ssc", tag="big1", align_bytes=64)
+            for b in range(3):
+                s_ps = psum.tile([P, 512], F32, name="s_ps%d" % b, tag="b%d" % b)
+                for i in range(4):
+                    nc.tensor.transpose(out=s_ps[:, P * i:P * i + P], in_=st_sb[:, 4 * b + i, :], identity=ident)
+                if b == 1:
+                    nc.vector.tensor_scalar_mul(out=ssc[:, 512 * b:512 * b + 512], in0=s_ps, scalar1=small["rden"][:, 0:1])
+                else:
+                    nc.scalar.activation(out=ssc[:, 512 * b:512 * b + 512], in_=s_ps, func=ACT.Copy, scale=small["rden"][:, 0:1])
+            small["ssc"] = ssc
+
+        def do_proto():
+            rden = small["rden"]
+            ssc = small["ssc"]
+            proto = keep.tile([P, D], F32, name="proto")
+            p2parts = const.tile([P, 3], F32, name="p2parts")
+            for n in range(3):
+                cols = slice(512 * n, 512 * n + 512)
+                nc.vector.scalar_tensor_tensor(out=proto[:, cols], in0=wu[n], scalar=rden[:, 0:1], in1=ssc[:, cols],
+                                               op0=ALU.mult, op1=ALU.add)
+            pview = proto.rearrange("j (g u p e) -> j g u e p", g=3, u=2, p=P, e=2)
+            pg = keep.tile([P, 3, C, 4], BF16, name="pg", align_bytes=64)
+            p_codes = keep.tile([P, 3, C], U32, name="p_codes", align_bytes=64)
+            p_scales = keep.tile([P, 3, C], U8, name="p_scales", align_bytes=64)
+            for g in range(3):
+                pt = psum.tile([P, 4, C], F32, name="pt%d" % g, tag="b%d" % g)
+                for u in range(2):
+                    for e in range(2):
+                        nc.tensor.transpose(out=pt[:, 2 * u + e, :], in_=pview[:, g, u, e, :], identity=ident)
+                cp = nc.scalar.copy if g == 1 else nc.vector.tensor_copy
+                cp(out=pg[:, g], in_=pt.rearrange("p t j -> p j t"))
+            for g in range(3):
+                nc.vector.quantize_mx(out=p_codes[:, g, :].bitcast(FP8X4), scales=p_scales[:, g, :],
+                                      in_=pg[:, g].rearrange("p j t -> p (j t)"))
+            for n in range(3):
+                cols = slice(512 * n, 512 * n + 512)
+                nc.scalar.activation(out=junk[:, cols], in_=proto[:, cols], func=ACT.Square,
+                                     accum_out=p2parts[:, n:n + 1])
+            p2 = const.tile([P, 1], F32, name="p2")
+            nc.vector.tensor_reduce(out=p2, in_=p2parts, axis=AX.X, op=ALU.add)
+            p2b_ps = psum.tile([P, C], F32, name="p2b_ps", tag="a0")
+            nc.tensor.matmul(out=p2b_ps, lhsT=p2[:, 0:1].to_broadcast([P, P]), rhs=ident, start=True, stop=True)
+            p2b = keep.tile([P, C], F32, name="p2b")
+            nc.scalar.copy(out=p2b, in_=p2b_ps)
+            small["p2b"] = p2b
+            small["p_codes"] = p_codes
+            small["p_scales"] = p_scales
+
+        def do_q(k, q_sb):
+            words = q_sb.bitcast(F32)
+            qg = stream.tile([P, 3 * 256 * 4], BF16, name="qg", tag="qg", bufs=2, align_bytes=64)
+            qg_w = qg.bitcast(F32)
+            for g in range(3):
+                xt = psum.tile([P, 2, 2, P], F32, name="xt", tag="xt", bufs=2)
+                for tt in range(2):
+                    for u in range(2):
+                        lo = 768 * tt + 256 * g + 128 * u
+                        nc.tensor.transpose(out=xt[:, tt, u, :], in_=words[:, lo:lo + 128], identity=ident)
+                nc.scalar.copy(out=qg_w[:, 512 * g:512 * g + 512].rearrange("p (t i u) -> p t i u", t=2, u=2),
+                               in_=xt.rearrange("p t u i -> p t i u"))
+            for tt in range(2):
+                nc.scalar.activation(out=junk, in_=q_sb[:, D * tt:D * tt + D], func=ACT.Square,
+                                     accum_out=q2[:, 2 * k + tt:2 * k + tt + 1])
+            for g in range(3):
+                nc.vector.quantize_mx(out=q_codes[:, g, 256 * k:256 * k + 256].bitcast(FP8X4),
+                                      scales=q_scales[:, g, 256 * k:256 * k + 256],
+                                      in_=qg[:, 1024 * g:1024 * g + 1024])
+
+        cr_tags = ["a1", "a2", "b0", "b1", "b2"]
+
+        def do_cross(k):
+            cr = psum.tile([P, 2, C], F32, name="cr", tag=cr_tags[k % len(cr_tags)])
+            for tt in range(2):
+                cols = slice(P * (2 * k + tt), P * (2 * k + tt) + P)
+                for g in range(3):
+                    nc.tensor.matmul_mx(out=cr[:, tt, :], lhsT=q_codes[:, g, cols].bitcast(FP8X4),
+                                        lhsT_scale=q_scales[:, g, cols],
+                                        rhs=small["p_codes"][:, g, :].bitcast(FP8X4),
+                                        rhs_scale=small["p_scales"][:, g, :],
+                                        start=(g == 0), stop=(g == 2))
+            nb = stream.tile([P, 2, C], F32, name="nb", tag="nb", bufs=2)
+            nc.vector.tensor_tensor(out=nb, in0=small["p2b"].unsqueeze(1).to_broadcast([P, 2, C]),
+                                    in1=q2[:, 2 * k:2 * k + 2].unsqueeze(2).to_broadcast([P, 2, C]), op=ALU.add)
+            nc.vector.scalar_tensor_tensor(out=o_sb[:, 2 * k:2 * k + 2, :].rearrange("p t j -> p (t j)"),
+                                           in0=cr.rearrange("p t j -> p (t j)"), scalar=2.0,
+                                           in1=nb.rearrange("p t j -> p (t j)"), op0=ALU.mult, op1=ALU.subtract)
+            if k % 2 == 1:
+                nc.sync.dma_start(out=out_dram[:, 2 * k - 2:2 * k + 2, :], in_=o_sb[:, 2 * k - 2:2 * k + 2, :])
+
+        pending = []
+        left = {"X": 8, "Z": 4}
+        load_ahead()
+        for it in items:
+            kind, idx = it[0], int(it[1:])
+            if kind == "W":
+                do_w(raw[it])
+            elif kind == "X":
+                do_x3(idx, raw[it])
+            elif kind == "Z":
+                do_x2(idx, raw[it])
+            else:
+                do_q(idx, raw[it])
+                pending.append(idx)
+            held[kind] -= 1
+            load_ahead()
+            if kind == "Z":
+                left["Z"] -= 1
+                if left["Z"] == 0:
+                    finish_x2()
+            if kind == "X":
+                left["X"] -= 1
+                if left["X"] == 0:
+                    do_proto()
+            if left["X"] == 0 and left["Z"] == 0:
+                for k in pending:
+                    do_cross(k)
+                pending = []

@@ -1,8 +1,6 @@
 from contextlib import ExitStack
 
-import concourse.bass as bass
 import concourse.mybir as mybir
-import concourse.tile as tile
 from concourse.masks import make_identity
 
 F32 = mybir.dt.float32
@@ -18,7 +16,52 @@ P = 128
 B, D, C, SHOT, U = 2048, 1536, 128, 16, 4096
 FLOPS = 2 * U * C * D + 2 * B * C * D
 
-S_COLS = 192
+ORDER = [
+    ("LD", "W", 0), ("LD", "Q", 0), ("LD", "X", 0), ("LD", "Q", 1), ("LD", "Q", 2), ("LD", "X", 1),
+    ("LD", "X", 2), ("LD", "Q", 3), ("LD", "Q", 4), ("WR", 0, "V"), ("WR", 1, "S"), ("DEN",),
+    ("WQ", 0), ("QT", 0, 0), ("QT", 0, 1), ("DENV",), ("QE", 0, 0, "S"), ("WQ", 1),
+    ("QE", 0, 1, "S"), ("QQ", 0, 0), ("QT", 0, 2), ("QE", 0, 2, "S"), ("QQ", 0, 1), ("QS", 0, 0, "S"),
+    ("QQ", 0, 2), ("XR", 0, 0, 512, "V"), ("XR", 0, 512, 1024, "V"), ("XR", 0, 1344, 1536, "S"), ("QT", 1, 0), ("QT", 1, 1),
+    ("QE", 1, 0, "S"), ("XR", 0, 1024, 1344, "V"), ("QS", 0, 1, "S"), ("QT", 1, 2), ("XQ", 0, 0), ("LD", "X", 3),
+    ("XQ", 0, 1), ("XM", 0, 0), ("XQ", 0, 2), ("XM", 0, 1), ("QE", 1, 1, "S"), ("QQ", 1, 0),
+    ("XM", 0, 2), ("QE", 1, 2, "S"), ("QQ", 1, 1), ("QT", 2, 0), ("QE", 2, 0, "S"), ("QQ", 1, 2),
+    ("QT", 2, 1), ("XR", 1, 1344, 1536, "S"), ("XR", 1, 0, 512, "V"), ("QT", 2, 2), ("QE", 2, 1, "S"), ("XR", 1, 512, 1024, "V"),
+    ("QS", 1, 0, "S"), ("XR", 1, 1024, 1344, "V"), ("LD", "X", 4), ("XR", 2, 0, 512, "V"), ("XR", 2, 1344, 1536, "S"), ("LD", "Z", 0),
+    ("LD", "Q", 5), ("LD", "Z", 1), ("QS", 1, 1, "S"), ("XR", 2, 512, 1024, "V"), ("QT", 3, 0), ("XR", 2, 1024, 1344, "V"),
+    ("QE", 2, 2, "S"), ("XQ", 1, 0), ("LD", "X", 5), ("QE", 3, 0, "S"), ("LD", "Q", 6), ("QT", 3, 1),
+    ("XQ", 1, 1), ("XM", 1, 0), ("QS", 2, 0, "S"), ("QT", 3, 2), ("XQ", 1, 2), ("XM", 1, 1),
+    ("XQ", 2, 0), ("XM", 1, 2), ("XQ", 2, 1), ("QS", 2, 1, "S"), ("XM", 2, 0), ("XQ", 2, 2),
+    ("XM", 2, 1), ("XR", 3, 0, 512, "V"), ("XM", 2, 2), ("XR", 3, 1344, 1536, "S"), ("XR", 3, 512, 1024, "V"), ("QE", 3, 1, "S"),
+    ("QE", 3, 2, "S"), ("QT", 4, 0), ("XR", 3, 1024, 1344, "V"), ("QS", 3, 0, "S"), ("QT", 4, 1), ("XR", 4, 0, 512, "V"),
+    ("LD", "X", 6), ("XR", 4, 512, 1024, "V"), ("XR", 4, 1344, 1536, "S"), ("QS", 3, 1, "S"), ("XR", 4, 1024, 1344, "V"), ("ZM", 0, 0),
+    ("XQ", 3, 0), ("XQ", 3, 1), ("XM", 3, 0), ("QS", 4, 0, "S"), ("ZM", 0, 1), ("XQ", 3, 2),
+    ("XM", 3, 1), ("QQ", 2, 0), ("XM", 3, 2), ("QQ", 2, 1), ("ZM", 0, 2), ("QQ", 2, 2),
+    ("QS", 4, 1, "S"), ("XQ", 4, 0), ("LD", "Z", 2), ("LD", "X", 7), ("XQ", 4, 1), ("XM", 4, 0),
+    ("LD", "Q", 7), ("XQ", 4, 2), ("XM", 4, 1), ("QE", 4, 0, "S"), ("QQ", 3, 0), ("ZM", 1, 0),
+    ("QE", 4, 1, "S"), ("QQ", 3, 1), ("QQ", 3, 2), ("QS", 5, 0, "S"), ("ZM", 1, 1), ("QQ", 4, 0),
+    ("QQ", 4, 1), ("ZM", 1, 2), ("QT", 4, 2), ("LD", "Z", 3), ("QS", 5, 1, "S"), ("QT", 5, 0),
+    ("XM", 4, 2), ("XR", 5, 0, 512, "V"), ("XR", 5, 1344, 1536, "S"), ("XR", 5, 512, 1024, "V"), ("QE", 4, 2, "S"), ("XR", 5, 1024, 1344, "V"),
+    ("QE", 5, 0, "S"), ("QT", 5, 1), ("XQ", 5, 0), ("QE", 5, 1, "S"), ("QT", 5, 2), ("XQ", 5, 1),
+    ("QE", 5, 2, "S"), ("XM", 5, 0), ("QT", 6, 0), ("XQ", 5, 2), ("QS", 6, 0, "S"), ("XM", 5, 1),
+    ("QT", 6, 1), ("XR", 6, 0, 512, "V"), ("XM", 5, 2), ("XR", 6, 1344, 1536, "S"), ("XR", 6, 512, 1024, "V"), ("QS", 6, 1, "S"),
+    ("XR", 6, 1024, 1344, "V"), ("ZM", 2, 0), ("XQ", 6, 0), ("XQ", 6, 1), ("XM", 6, 0), ("ZM", 2, 1),
+    ("XQ", 6, 2), ("QQ", 4, 2), ("XM", 6, 1), ("QQ", 5, 0), ("XM", 6, 2), ("QE", 6, 0, "S"),
+    ("ZM", 2, 2), ("QQ", 5, 1), ("QQ", 5, 2), ("QE", 6, 1, "S"), ("XR", 7, 0, 512, "V"), ("QT", 6, 2),
+    ("XR", 7, 1344, 1536, "S"), ("QE", 6, 2, "S"), ("XR", 7, 512, 1024, "V"), ("QT", 7, 0), ("QS", 7, 0, "S"), ("QT", 7, 1),
+    ("XR", 7, 1024, 1344, "V"), ("XQ", 7, 0), ("QE", 7, 0, "S"), ("XQ", 7, 1), ("XM", 7, 0), ("QS", 7, 1, "S"),
+    ("QT", 7, 2), ("XQ", 7, 2), ("XM", 7, 1), ("ZM", 3, 0), ("QQ", 6, 0), ("QQ", 6, 1),
+    ("QQ", 6, 2), ("ZM", 3, 1), ("SE", 0, "S"), ("QQ", 7, 0), ("QE", 7, 1, "S"), ("ZM", 3, 2),
+    ("SE", 1, "V"), ("QE", 7, 2, "S"), ("QQ", 7, 1), ("STT", 0), ("SE", 2, "S"), ("STT", 1),
+    ("QQ", 7, 2), ("XM", 7, 2), ("SS", 1, "V"), ("SS", 0, "S"), ("STT", 2), ("PR", 1),
+    ("SS", 2, "S"), ("PR", 0), ("PT", 1), ("P2", 1), ("PR", 2), ("PT", 0),
+    ("P2", 0), ("PT", 2), ("PC", 0, "V"), ("P2", 2), ("PC", 2, "V"), ("PC", 1, "S"),
+    ("P2R",), ("PQ", 0), ("P2M",), ("PQ", 2), ("PQ", 1), ("P2C",),
+    ("CR", 0), ("NB", 0, "V"), ("NB", 1, "V"), ("CR", 1), ("NB", 2, "V"), ("CR", 2),
+    ("NB", 3, "V"), ("CR", 3), ("EP", 0), ("EP", 1), ("CR", 4), ("EP", 2),
+    ("OUT", 1), ("CR", 5), ("EP", 3), ("CR", 6), ("NB", 4, "V"), ("OUT", 3),
+    ("NB", 5, "V"), ("CR", 7), ("NB", 6, "V"), ("NB", 7, "V"), ("EP", 4), ("EP", 5),
+    ("EP", 6), ("OUT", 5), ("EP", 7), ("OUT", 7),
+]
 
 
 def tile_proto_metric_semi_kernel(tc, x1, x2, x3, w, out):
@@ -34,6 +77,7 @@ def tile_proto_metric_semi_kernel(tc, x1, x2, x3, w, out):
         keep = ctx.enter_context(tc.tile_pool(name="keep", bufs=1))
         stream = ctx.enter_context(tc.tile_pool(name="stream", bufs=2))
         psum = ctx.enter_context(tc.psum_pool(name="psum", bufs=1))
+        ctx.enter_context(tc.manual_schedule())
 
         ident = const.tile([P, P], F32, name="ident")
         make_identity(nc, ident)
@@ -52,215 +96,199 @@ def tile_proto_metric_semi_kernel(tc, x1, x2, x3, w, out):
         w_codes = keep.tile([P, 8 * C], U32, name="w_codes", align_bytes=64)
         w_scales = keep.tile([P, 8 * C], U8, name="w_scales", align_bytes=64)
 
-        items = ["W0", "X0", "Q0", "X1", "Q1", "X2", "Z0", "Q2", "X3", "Z1", "Q3", "X4", "Z2", "Q4",
-                 "X5", "Z3", "Q5", "X6", "X7", "Q6", "Q7"]
-        depth = {"W": 1, "X": 3, "Q": 5, "Z": 2}
-        held = {"W": 0, "X": 0, "Q": 0, "Z": 0}
-        raw = {}
-        state = {"next": 0}
+        T = {}
+        cr_tags = ["a1", "a2", "b0", "b1"]
 
-        def load_ahead():
-            while state["next"] < len(items):
-                it = items[state["next"]]
-                kind, idx = it[0], int(it[1:])
-                if held[kind] >= depth[kind]:
-                    break
+        def copier(eng):
+            return nc.vector.tensor_copy if eng == "V" else nc.scalar.copy
+
+        for tok in ORDER:
+            op = tok[0]
+            if op == "LD":
+                kind, i = tok[1], tok[2]
                 if kind == "W":
                     t = keep.tile([P, 8, 4, C], BF16, name="w_sb", tag="big0")
                     nc.sync.dma_start(out=t, in_=w_dram)
                 elif kind == "X":
                     t = stream.tile([P, 4, D], BF16, name="x3raw", tag="x3raw", bufs=3)
-                    nc.sync.dma_start(out=t, in_=x3_dram[idx])
+                    nc.sync.dma_start(out=t, in_=x3_dram[i])
                 elif kind == "Z":
                     t = stream.tile([P, 4, D], BF16, name="x2raw", tag="x2raw", bufs=2)
-                    nc.sync.dma_start(out=t, in_=x2_dram[idx])
+                    nc.sync.dma_start(out=t, in_=x2_dram[i])
                 else:
                     t = stream.tile([P, 2 * D], BF16, name="qraw", tag="qraw", bufs=5)
-                    nc.sync.dma_start(out=t.rearrange("p (t d) -> p t d", t=2), in_=q_dram[:, 2 * idx:2 * idx + 2, :])
-                raw[it] = t
-                held[kind] += 1
-                state["next"] += 1
-
-        small = {}
-        wu = []
-        st = []
-
-        def do_w(w_sb):
-            w_g = keep.tile([P, 8, C, 4], BF16, name="w_g", tag="big1", align_bytes=64)
-            for h in range(2):
-                nc.vector.tensor_copy(out=w_g[:, 4 * h:4 * h + 4], in_=w_sb[:, 4 * h:4 * h + 4].rearrange("p c j m -> p c m j"))
-            for h in range(2):
-                nc.vector.quantize_mx(
-                    out=w_codes[:, 512 * h:512 * h + 512].bitcast(FP8X4),
-                    scales=w_scales[:, 512 * h:512 * h + 512],
-                    in_=w_g[:, 4 * h:4 * h + 4].rearrange("p c m j -> p (c m j)"),
-                )
-            den_ps = psum.tile([P, 2], F32, name="den_ps", tag="b0")
-            for c in range(8):
-                for j in range(4):
-                    nc.tensor.matmul(out=den_ps, lhsT=w_sb[:, c, j, :], rhs=ones,
-                                     start=(c == 0 and j == 0), stop=(c == 7 and j == 3))
-            den = const.tile([P, 1], F32, name="den")
-            nc.vector.tensor_scalar_add(out=den, in0=den_ps[:, 0:1], scalar1=float(SHOT))
-            rden = const.tile([P, 1], F32, name="rden")
-            nc.vector.reciprocal(out=rden, in_=den)
-            small["rden"] = rden
-
-        def regroup(copy, dst, src, lo, hi):
-            copy(out=dst[:, lo:hi, :].rearrange("p (c i) t -> p c t i", i=4),
-                 in_=src[:, :, lo:hi].rearrange("p t (c i) -> p c t i", i=4))
-
-        def do_x3(c, x_sb):
-            if c == 0:
-                for n in range(3):
-                    wu.append(psum.tile([P, 512], F32, name="wu%d" % n, tag="a%d" % n))
-            g = stream.tile([P, D, 4], BF16, name="x3g", tag="x3g", bufs=2, align_bytes=64)
-            codes = stream.tile([P, D], U32, name="x3c", tag="x3c", bufs=2, align_bytes=64)
-            scales = stream.tile([P, D], U8, name="x3s", tag="x3s", bufs=2, align_bytes=64)
-            regroup(nc.scalar.copy, g, x_sb, D - S_COLS, D)
-            regroup(nc.vector.tensor_copy, g, x_sb, 0, 512)
-            regroup(nc.vector.tensor_copy, g, x_sb, 512, 1024)
-            regroup(nc.vector.tensor_copy, g, x_sb, 1024, D - S_COLS)
-            for n in range(3):
+                    nc.sync.dma_start(out=t.rearrange("p (t d) -> p t d", t=2), in_=q_dram[:, 2 * i:2 * i + 2, :])
+                T[(kind, i)] = t
+            elif op == "WR":
+                h = tok[1]
+                if "w_g" not in T:
+                    T["w_g"] = keep.tile([P, 8, C, 4], BF16, name="w_g", tag="big1", align_bytes=64)
+                copier(tok[2])(out=T["w_g"][:, 4 * h:4 * h + 4],
+                               in_=T[("W", 0)][:, 4 * h:4 * h + 4].rearrange("p c j m -> p c m j"))
+            elif op == "WQ":
+                h = tok[1]
+                nc.vector.quantize_mx(out=w_codes[:, 512 * h:512 * h + 512].bitcast(FP8X4),
+                                      scales=w_scales[:, 512 * h:512 * h + 512],
+                                      in_=T["w_g"][:, 4 * h:4 * h + 4].rearrange("p c m j -> p (c m j)"))
+            elif op == "DEN":
+                T["den_ps"] = psum.tile([P, 2], F32, name="den_ps", tag="b0")
+                for c in range(8):
+                    for j in range(4):
+                        nc.tensor.matmul(out=T["den_ps"], lhsT=T[("W", 0)][:, c, j, :], rhs=ones,
+                                         start=(c == 0 and j == 0), stop=(c == 7 and j == 3))
+            elif op == "DENV":
+                den = const.tile([P, 1], F32, name="den")
+                nc.vector.tensor_scalar_add(out=den, in0=T["den_ps"][:, 0:1], scalar1=float(SHOT))
+                T["rden"] = const.tile([P, 1], F32, name="rden")
+                nc.vector.reciprocal(out=T["rden"], in_=den)
+            elif op == "XR":
+                c, lo, hi = tok[1], tok[2], tok[3]
+                if ("g", c) not in T:
+                    T[("g", c)] = stream.tile([P, D, 4], BF16, name="x3g", tag="x3g", bufs=2, align_bytes=64)
+                copier(tok[4])(out=T[("g", c)][:, lo:hi, :].rearrange("p (c i) t -> p c t i", i=4),
+                               in_=T[("X", c)][:, :, lo:hi].rearrange("p t (c i) -> p c t i", i=4))
+            elif op == "XQ":
+                c, n = tok[1], tok[2]
+                if ("c", c) not in T:
+                    T[("c", c)] = stream.tile([P, D], U32, name="x3c", tag="x3c", bufs=2, align_bytes=64)
+                    T[("s", c)] = stream.tile([P, D], U8, name="x3s", tag="x3s", bufs=2, align_bytes=64)
                 cols = slice(512 * n, 512 * n + 512)
-                nc.vector.quantize_mx(out=codes[:, cols].bitcast(FP8X4), scales=scales[:, cols],
-                                      in_=g[:, cols, :].rearrange("p c t -> p (c t)"))
-            for n in range(3):
+                nc.vector.quantize_mx(out=T[("c", c)][:, cols].bitcast(FP8X4), scales=T[("s", c)][:, cols],
+                                      in_=T[("g", c)][:, cols, :].rearrange("p c t -> p (c t)"))
+            elif op == "XM":
+                c, n = tok[1], tok[2]
+                if ("wu", n) not in T:
+                    T[("wu", n)] = psum.tile([P, 512], F32, name="wu%d" % n, tag="a%d" % n)
                 cols = slice(512 * n, 512 * n + 512)
-                nc.tensor.matmul_mx(out=wu[n], lhsT=w_codes[:, C * c:C * c + C].bitcast(FP8X4),
+                nc.tensor.matmul_mx(out=T[("wu", n)], lhsT=w_codes[:, C * c:C * c + C].bitcast(FP8X4),
                                     lhsT_scale=w_scales[:, C * c:C * c + C],
-                                    rhs=codes[:, cols].bitcast(FP8X4), rhs_scale=scales[:, cols],
+                                    rhs=T[("c", c)][:, cols].bitcast(FP8X4), rhs_scale=T[("s", c)][:, cols],
                                     start=(c == 0), stop=(c == 7))
-
-        def do_x2(h, z_sb):
-            if h == 0:
-                for b in range(3):
-                    st.append(psum.tile([P, 4, C], F32, name="st%d" % b, tag="b%d" % b))
-            for dt in range(12):
-                for s in range(4):
-                    nc.tensor.matmul(out=st[dt // 4][:, dt % 4, 32 * h:32 * h + 32],
-                                     lhsT=z_sb[:, s, P * dt:P * dt + P], rhs=sel,
-                                     start=(s == 0), stop=(s == 3))
-
-        def finish_x2():
-            st_sb = keep.tile([P, 12, C], F32, name="st_sb", tag="big0")
-            for b in range(3):
-                cp = nc.vector.tensor_copy if b == 1 else nc.scalar.copy
-                cp(out=st_sb[:, 4 * b:4 * b + 4, :], in_=st[b])
-            ssc = keep.tile([P, D], F32, name="ssc", tag="big1", align_bytes=64)
-            for b in range(3):
-                s_ps = psum.tile([P, 512], F32, name="s_ps%d" % b, tag="b%d" % b)
+            elif op == "ZM":
+                h, b = tok[1], tok[2]
+                if ("st", b) not in T:
+                    T[("st", b)] = psum.tile([P, 4, C], F32, name="st%d" % b, tag="b%d" % b)
                 for i in range(4):
-                    nc.tensor.transpose(out=s_ps[:, P * i:P * i + P], in_=st_sb[:, 4 * b + i, :], identity=ident)
-                if b == 1:
-                    nc.vector.tensor_scalar_mul(out=ssc[:, 512 * b:512 * b + 512], in0=s_ps, scalar1=small["rden"][:, 0:1])
+                    for s in range(4):
+                        lo = P * (4 * b + i)
+                        nc.tensor.matmul(out=T[("st", b)][:, i, 32 * h:32 * h + 32],
+                                         lhsT=T[("Z", h)][:, s, lo:lo + P], rhs=sel,
+                                         start=(s == 0), stop=(s == 3))
+            elif op == "SE":
+                b = tok[1]
+                if "st_sb" not in T:
+                    T["st_sb"] = keep.tile([P, 12, C], F32, name="st_sb", tag="big0")
+                copier(tok[2])(out=T["st_sb"][:, 4 * b:4 * b + 4, :], in_=T[("st", b)])
+            elif op == "STT":
+                b = tok[1]
+                T[("s_ps", b)] = psum.tile([P, 512], F32, name="s_ps%d" % b, tag="b%d" % b)
+                for i in range(4):
+                    nc.tensor.transpose(out=T[("s_ps", b)][:, P * i:P * i + P], in_=T["st_sb"][:, 4 * b + i, :],
+                                        identity=ident)
+            elif op == "SS":
+                b = tok[1]
+                if "ssc" not in T:
+                    T["ssc"] = keep.tile([P, D], F32, name="ssc", tag="big1", align_bytes=64)
+                cols = slice(512 * b, 512 * b + 512)
+                if tok[2] == "V":
+                    nc.vector.tensor_scalar_mul(out=T["ssc"][:, cols], in0=T[("s_ps", b)], scalar1=T["rden"][:, 0:1])
                 else:
-                    nc.scalar.activation(out=ssc[:, 512 * b:512 * b + 512], in_=s_ps, func=ACT.Copy, scale=small["rden"][:, 0:1])
-            small["ssc"] = ssc
-
-        def do_proto():
-            rden = small["rden"]
-            ssc = small["ssc"]
-            proto = keep.tile([P, D], F32, name="proto")
-            p2parts = const.tile([P, 3], F32, name="p2parts")
-            for n in range(3):
+                    nc.scalar.activation(out=T["ssc"][:, cols], in_=T[("s_ps", b)], func=ACT.Copy,
+                                         scale=T["rden"][:, 0:1])
+            elif op == "PR":
+                n = tok[1]
+                if "proto" not in T:
+                    T["proto"] = keep.tile([P, D], F32, name="proto")
                 cols = slice(512 * n, 512 * n + 512)
-                nc.vector.scalar_tensor_tensor(out=proto[:, cols], in0=wu[n], scalar=rden[:, 0:1], in1=ssc[:, cols],
-                                               op0=ALU.mult, op1=ALU.add)
-            pview = proto.rearrange("j (g u p e) -> j g u e p", g=3, u=2, p=P, e=2)
-            pg = keep.tile([P, 3, C, 4], BF16, name="pg", align_bytes=64)
-            p_codes = keep.tile([P, 3, C], U32, name="p_codes", align_bytes=64)
-            p_scales = keep.tile([P, 3, C], U8, name="p_scales", align_bytes=64)
-            for g in range(3):
-                pt = psum.tile([P, 4, C], F32, name="pt%d" % g, tag="b%d" % g)
+                nc.vector.scalar_tensor_tensor(out=T["proto"][:, cols], in0=T[("wu", n)], scalar=T["rden"][:, 0:1],
+                                               in1=T["ssc"][:, cols], op0=ALU.mult, op1=ALU.add)
+            elif op == "PT":
+                g = tok[1]
+                pview = T["proto"].rearrange("j (g u p e) -> j g u e p", g=3, u=2, p=P, e=2)
+                T[("pt", g)] = psum.tile([P, 4, C], F32, name="pt%d" % g, tag="b%d" % g)
                 for u in range(2):
                     for e in range(2):
-                        nc.tensor.transpose(out=pt[:, 2 * u + e, :], in_=pview[:, g, u, e, :], identity=ident)
-                cp = nc.scalar.copy if g == 1 else nc.vector.tensor_copy
-                cp(out=pg[:, g], in_=pt.rearrange("p t j -> p j t"))
-            for g in range(3):
-                nc.vector.quantize_mx(out=p_codes[:, g, :].bitcast(FP8X4), scales=p_scales[:, g, :],
-                                      in_=pg[:, g].rearrange("p j t -> p (j t)"))
-            for n in range(3):
+                        nc.tensor.transpose(out=T[("pt", g)][:, 2 * u + e, :], in_=pview[:, g, u, e, :], identity=ident)
+            elif op == "PC":
+                g = tok[1]
+                if "pg" not in T:
+                    T["pg"] = keep.tile([P, 3, C, 4], BF16, name="pg", align_bytes=64)
+                copier(tok[2])(out=T["pg"][:, g], in_=T[("pt", g)].rearrange("p t j -> p j t"))
+            elif op == "PQ":
+                g = tok[1]
+                if "p_codes" not in T:
+                    T["p_codes"] = keep.tile([P, 3, C], U32, name="p_codes", align_bytes=64)
+                    T["p_scales"] = keep.tile([P, 3, C], U8, name="p_scales", align_bytes=64)
+                nc.vector.quantize_mx(out=T["p_codes"][:, g, :].bitcast(FP8X4), scales=T["p_scales"][:, g, :],
+                                      in_=T["pg"][:, g].rearrange("p j t -> p (j t)"))
+            elif op == "P2":
+                n = tok[1]
+                if "p2parts" not in T:
+                    T["p2parts"] = const.tile([P, 3], F32, name="p2parts")
                 cols = slice(512 * n, 512 * n + 512)
-                nc.scalar.activation(out=junk[:, cols], in_=proto[:, cols], func=ACT.Square,
-                                     accum_out=p2parts[:, n:n + 1])
-            p2 = const.tile([P, 1], F32, name="p2")
-            nc.vector.tensor_reduce(out=p2, in_=p2parts, axis=AX.X, op=ALU.add)
-            p2b_ps = psum.tile([P, C], F32, name="p2b_ps", tag="a0")
-            nc.tensor.matmul(out=p2b_ps, lhsT=p2[:, 0:1].to_broadcast([P, P]), rhs=ident, start=True, stop=True)
-            p2b = keep.tile([P, C], F32, name="p2b")
-            nc.scalar.copy(out=p2b, in_=p2b_ps)
-            small["p2b"] = p2b
-            small["p_codes"] = p_codes
-            small["p_scales"] = p_scales
-
-        def do_q(k, q_sb):
-            words = q_sb.bitcast(F32)
-            qg = stream.tile([P, 3 * 256 * 4], BF16, name="qg", tag="qg", bufs=2, align_bytes=64)
-            qg_w = qg.bitcast(F32)
-            for g in range(3):
+                nc.scalar.activation(out=junk[:, cols], in_=T["proto"][:, cols], func=ACT.Square,
+                                     accum_out=T["p2parts"][:, n:n + 1])
+            elif op == "P2R":
+                T["p2"] = const.tile([P, 1], F32, name="p2")
+                nc.vector.tensor_reduce(out=T["p2"], in_=T["p2parts"], axis=AX.X, op=ALU.add)
+            elif op == "P2M":
+                T["p2b_ps"] = psum.tile([P, C], F32, name="p2b_ps", tag="a0")
+                nc.tensor.matmul(out=T["p2b_ps"], lhsT=T["p2"][:, 0:1].to_broadcast([P, P]), rhs=ident,
+                                 start=True, stop=True)
+            elif op == "P2C":
+                T["p2b"] = keep.tile([P, C], F32, name="p2b")
+                nc.scalar.copy(out=T["p2b"], in_=T["p2b_ps"])
+            elif op == "QT":
+                k, g = tok[1], tok[2]
+                words = T[("Q", k)].bitcast(F32)
                 xt = psum.tile([P, 2, 2, P], F32, name="xt", tag="xt", bufs=2)
+                T[("xt", k, g)] = xt
                 for tt in range(2):
                     for u in range(2):
                         lo = 768 * tt + 256 * g + 128 * u
                         nc.tensor.transpose(out=xt[:, tt, u, :], in_=words[:, lo:lo + 128], identity=ident)
-                nc.scalar.copy(out=qg_w[:, 512 * g:512 * g + 512].rearrange("p (t i u) -> p t i u", t=2, u=2),
-                               in_=xt.rearrange("p t u i -> p t i u"))
-            for tt in range(2):
-                nc.scalar.activation(out=junk, in_=q_sb[:, D * tt:D * tt + D], func=ACT.Square,
+            elif op == "QE":
+                k, g = tok[1], tok[2]
+                if ("qg", k) not in T:
+                    T[("qg", k)] = stream.tile([P, 3 * 256 * 4], BF16, name="qg", tag="qg", bufs=2, align_bytes=64)
+                qg_w = T[("qg", k)].bitcast(F32)
+                copier(tok[3])(out=qg_w[:, 512 * g:512 * g + 512].rearrange("p (t i u) -> p t i u", t=2, u=2),
+                               in_=T[("xt", k, g)].rearrange("p t u i -> p t i u"))
+            elif op == "QS":
+                k, tt = tok[1], tok[2]
+                nc.scalar.activation(out=junk, in_=T[("Q", k)][:, D * tt:D * tt + D], func=ACT.Square,
                                      accum_out=q2[:, 2 * k + tt:2 * k + tt + 1])
-            for g in range(3):
+            elif op == "QQ":
+                k, g = tok[1], tok[2]
                 nc.vector.quantize_mx(out=q_codes[:, g, 256 * k:256 * k + 256].bitcast(FP8X4),
                                       scales=q_scales[:, g, 256 * k:256 * k + 256],
-                                      in_=qg[:, 1024 * g:1024 * g + 1024])
-
-        cr_tags = ["a1", "a2", "b0", "b1", "b2"]
-
-        def do_cross(k):
-            cr = psum.tile([P, 2, C], F32, name="cr", tag=cr_tags[k % len(cr_tags)])
-            for tt in range(2):
-                cols = slice(P * (2 * k + tt), P * (2 * k + tt) + P)
-                for g in range(3):
-                    nc.tensor.matmul_mx(out=cr[:, tt, :], lhsT=q_codes[:, g, cols].bitcast(FP8X4),
-                                        lhsT_scale=q_scales[:, g, cols],
-                                        rhs=small["p_codes"][:, g, :].bitcast(FP8X4),
-                                        rhs_scale=small["p_scales"][:, g, :],
-                                        start=(g == 0), stop=(g == 2))
-            nb = stream.tile([P, 2, C], F32, name="nb", tag="nb", bufs=2)
-            nc.vector.tensor_tensor(out=nb, in0=small["p2b"].unsqueeze(1).to_broadcast([P, 2, C]),
-                                    in1=q2[:, 2 * k:2 * k + 2].unsqueeze(2).to_broadcast([P, 2, C]), op=ALU.add)
-            nc.vector.scalar_tensor_tensor(out=o_sb[:, 2 * k:2 * k + 2, :].rearrange("p t j -> p (t j)"),
-                                           in0=cr.rearrange("p t j -> p (t j)"), scalar=2.0,
-                                           in1=nb.rearrange("p t j -> p (t j)"), op0=ALU.mult, op1=ALU.subtract)
-            if k % 2 == 1:
+                                      in_=T[("qg", k)][:, 1024 * g:1024 * g + 1024])
+            elif op == "NB":
+                k = tok[1]
+                T[("nb", k)] = stream.tile([P, 2, C], F32, name="nb", tag="nb", bufs=8)
+                eng = nc.vector if tok[2] == "V" else nc.gpsimd
+                eng.tensor_tensor(out=T[("nb", k)], in0=T["p2b"].unsqueeze(1).to_broadcast([P, 2, C]),
+                                  in1=q2[:, 2 * k:2 * k + 2].unsqueeze(2).to_broadcast([P, 2, C]), op=ALU.add)
+            elif op == "CR":
+                k = tok[1]
+                cr = psum.tile([P, 2, C], F32, name="cr", tag=cr_tags[k % 4])
+                T[("cr", k)] = cr
+                for tt in range(2):
+                    cols = slice(P * (2 * k + tt), P * (2 * k + tt) + P)
+                    for g in range(3):
+                        nc.tensor.matmul_mx(out=cr[:, tt, :], lhsT=q_codes[:, g, cols].bitcast(FP8X4),
+                                            lhsT_scale=q_scales[:, g, cols],
+                                            rhs=T["p_codes"][:, g, :].bitcast(FP8X4),
+                                            rhs_scale=T["p_scales"][:, g, :],
+                                            start=(g == 0), stop=(g == 2))
+            elif op == "EP":
+                k = tok[1]
+                nc.vector.scalar_tensor_tensor(out=o_sb[:, 2 * k:2 * k + 2, :].rearrange("p t j -> p (t j)"),
+                                               in0=T[("cr", k)].rearrange("p t j -> p (t j)"), scalar=2.0,
+                                               in1=T[("nb", k)].rearrange("p t j -> p (t j)"),
+                                               op0=ALU.mult, op1=ALU.subtract)
+            elif op == "OUT":
+                k = tok[1]
                 nc.sync.dma_start(out=out_dram[:, 2 * k - 2:2 * k + 2, :], in_=o_sb[:, 2 * k - 2:2 * k + 2, :])
-
-        pending = []
-        left = {"X": 8, "Z": 4}
-        load_ahead()
-        for it in items:
-            kind, idx = it[0], int(it[1:])
-            if kind == "W":
-                do_w(raw[it])
-            elif kind == "X":
-                do_x3(idx, raw[it])
-            elif kind == "Z":
-                do_x2(idx, raw[it])
             else:
-                do_q(idx, raw[it])
-                pending.append(idx)
-            held[kind] -= 1
-            load_ahead()
-            if kind == "Z":
-                left["Z"] -= 1
-                if left["Z"] == 0:
-                    finish_x2()
-            if kind == "X":
-                left["X"] -= 1
-                if left["X"] == 0:
-                    do_proto()
-            if left["X"] == 0 and left["Z"] == 0:
-                for k in pending:
-                    do_cross(k)
-                pending = []
+                assert False, op

@@ -16,59 +16,32 @@ P = 128
 B, D, C, SHOT, U = 2048, 1536, 128, 16, 4096
 FLOPS = 2 * U * C * D + 2 * B * C * D
 
-ORDER = [
-    ("LD", "W", 0), ("LD", "Q", 0), ("LD", "X", 0), ("LD", "Q", 1), ("LD", "Q", 2), ("LD", "X", 1),
-    ("LD", "X", 2), ("LD", "Q", 3), ("LD", "Q", 4), ("WR", 0, "V"), ("WR", 1, "S"), ("DEN",),
-    ("WQ", 0), ("QT", 0, 0), ("QT", 0, 1), ("DENV",), ("QE", 0, 0, "S"), ("WQ", 1),
-    ("QE", 0, 1, "S"), ("QQ", 0, 0), ("QT", 0, 2), ("QE", 0, 2, "S"), ("QQ", 0, 1), ("QS", 0, 0, "S"),
-    ("QQ", 0, 2), ("XR", 0, 0, 512, "V"), ("XR", 0, 512, 1024, "V"), ("XR", 0, 1344, 1536, "S"), ("QT", 1, 0), ("QT", 1, 1),
-    ("QE", 1, 0, "S"), ("XR", 0, 1024, 1344, "V"), ("QS", 0, 1, "S"), ("QT", 1, 2), ("XQ", 0, 0), ("LD", "X", 3),
-    ("XQ", 0, 1), ("XM", 0, 0), ("XQ", 0, 2), ("XM", 0, 1), ("QE", 1, 1, "S"), ("QQ", 1, 0),
-    ("XM", 0, 2), ("QE", 1, 2, "S"), ("QQ", 1, 1), ("QT", 2, 0), ("QE", 2, 0, "S"), ("QQ", 1, 2),
-    ("QT", 2, 1), ("XR", 1, 1344, 1536, "S"), ("XR", 1, 0, 512, "V"), ("QT", 2, 2), ("QE", 2, 1, "S"), ("XR", 1, 512, 1024, "V"),
-    ("QS", 1, 0, "S"), ("XR", 1, 1024, 1344, "V"), ("LD", "X", 4), ("XR", 2, 0, 512, "V"), ("XR", 2, 1344, 1536, "S"), ("LD", "Z", 0),
-    ("LD", "Q", 5), ("LD", "Z", 1), ("QS", 1, 1, "S"), ("XR", 2, 512, 1024, "V"), ("QT", 3, 0), ("XR", 2, 1024, 1344, "V"),
-    ("QE", 2, 2, "S"), ("XQ", 1, 0), ("LD", "X", 5), ("QE", 3, 0, "S"), ("LD", "Q", 6), ("QT", 3, 1),
-    ("XQ", 1, 1), ("XM", 1, 0), ("QS", 2, 0, "S"), ("QT", 3, 2), ("XQ", 1, 2), ("XM", 1, 1),
-    ("XQ", 2, 0), ("XM", 1, 2), ("XQ", 2, 1), ("QS", 2, 1, "S"), ("XM", 2, 0), ("XQ", 2, 2),
-    ("XM", 2, 1), ("XR", 3, 0, 512, "V"), ("XM", 2, 2), ("XR", 3, 1344, 1536, "S"), ("XR", 3, 512, 1024, "V"), ("QE", 3, 1, "S"),
-    ("QE", 3, 2, "S"), ("QT", 4, 0), ("XR", 3, 1024, 1344, "V"), ("QS", 3, 0, "S"), ("QT", 4, 1), ("XR", 4, 0, 512, "V"),
-    ("LD", "X", 6), ("XR", 4, 512, 1024, "V"), ("XR", 4, 1344, 1536, "S"), ("QS", 3, 1, "S"), ("XR", 4, 1024, 1344, "V"), ("ZM", 0, 0),
-    ("XQ", 3, 0), ("XQ", 3, 1), ("XM", 3, 0), ("QS", 4, 0, "S"), ("ZM", 0, 1), ("XQ", 3, 2),
-    ("XM", 3, 1), ("QQ", 2, 0), ("XM", 3, 2), ("QQ", 2, 1), ("ZM", 0, 2), ("QQ", 2, 2),
-    ("QS", 4, 1, "S"), ("XQ", 4, 0), ("LD", "Z", 2), ("LD", "X", 7), ("XQ", 4, 1), ("XM", 4, 0),
-    ("LD", "Q", 7), ("XQ", 4, 2), ("XM", 4, 1), ("QE", 4, 0, "S"), ("QQ", 3, 0), ("ZM", 1, 0),
-    ("QE", 4, 1, "S"), ("QQ", 3, 1), ("QQ", 3, 2), ("QS", 5, 0, "S"), ("ZM", 1, 1), ("QQ", 4, 0),
-    ("QQ", 4, 1), ("ZM", 1, 2), ("QT", 4, 2), ("LD", "Z", 3), ("QS", 5, 1, "S"), ("QT", 5, 0),
-    ("XM", 4, 2), ("XR", 5, 0, 512, "V"), ("XR", 5, 1344, 1536, "S"), ("XR", 5, 512, 1024, "V"), ("QE", 4, 2, "S"), ("XR", 5, 1024, 1344, "V"),
-    ("QE", 5, 0, "S"), ("QT", 5, 1), ("XQ", 5, 0), ("QE", 5, 1, "S"), ("QT", 5, 2), ("XQ", 5, 1),
-    ("QE", 5, 2, "S"), ("XM", 5, 0), ("QT", 6, 0), ("XQ", 5, 2), ("QS", 6, 0, "S"), ("XM", 5, 1),
-    ("QT", 6, 1), ("XR", 6, 0, 512, "V"), ("XM", 5, 2), ("XR", 6, 1344, 1536, "S"), ("XR", 6, 512, 1024, "V"), ("QS", 6, 1, "S"),
-    ("XR", 6, 1024, 1344, "V"), ("ZM", 2, 0), ("XQ", 6, 0), ("XQ", 6, 1), ("XM", 6, 0), ("ZM", 2, 1),
-    ("XQ", 6, 2), ("QQ", 4, 2), ("XM", 6, 1), ("QQ", 5, 0), ("XM", 6, 2), ("QE", 6, 0, "S"),
-    ("ZM", 2, 2), ("QQ", 5, 1), ("QQ", 5, 2), ("QE", 6, 1, "S"), ("XR", 7, 0, 512, "V"), ("QT", 6, 2),
-    ("XR", 7, 1344, 1536, "S"), ("QE", 6, 2, "S"), ("XR", 7, 512, 1024, "V"), ("QT", 7, 0), ("QS", 7, 0, "S"), ("QT", 7, 1),
-    ("XR", 7, 1024, 1344, "V"), ("XQ", 7, 0), ("QE", 7, 0, "S"), ("XQ", 7, 1), ("XM", 7, 0), ("QS", 7, 1, "S"),
-    ("QT", 7, 2), ("XQ", 7, 2), ("XM", 7, 1), ("ZM", 3, 0), ("QQ", 6, 0), ("QQ", 6, 1),
-    ("QQ", 6, 2), ("ZM", 3, 1), ("SE", 0, "S"), ("QQ", 7, 0), ("QE", 7, 1, "S"), ("ZM", 3, 2),
-    ("SE", 1, "V"), ("QE", 7, 2, "S"), ("QQ", 7, 1), ("STT", 0), ("SE", 2, "S"), ("STT", 1),
-    ("QQ", 7, 2), ("XM", 7, 2), ("SS", 1, "V"), ("SS", 0, "S"), ("STT", 2), ("PR", 1),
-    ("SS", 2, "S"), ("PR", 0), ("PT", 1), ("P2", 1), ("PR", 2), ("PT", 0),
-    ("P2", 0), ("PT", 2), ("PC", 0, "V"), ("P2", 2), ("PC", 2, "V"), ("PC", 1, "S"),
-    ("P2R",), ("PQ", 0), ("P2M",), ("PQ", 2), ("PQ", 1), ("P2C",),
-    ("CR", 0), ("NB", 0, "V"), ("NB", 1, "V"), ("CR", 1), ("NB", 2, "V"), ("CR", 2),
-    ("NB", 3, "V"), ("CR", 3), ("EP", 0), ("EP", 1), ("CR", 4), ("EP", 2),
-    ("OUT", 1), ("CR", 5), ("EP", 3), ("CR", 6), ("NB", 4, "V"), ("OUT", 3),
-    ("NB", 5, "V"), ("CR", 7), ("NB", 6, "V"), ("NB", 7, "V"), ("EP", 4), ("EP", 5),
-    ("EP", 6), ("OUT", 5), ("EP", 7), ("OUT", 7),
-]
+ROUNDS = 8
+S_COLS = 64
+Z_OF_ROUND = {3: [0], 4: [1], 5: [2], 6: [3], 7: [4], 8: [5]}
+Z_TAIL = [6, 7]
+DEPTH = {"W": 1, "X": 3, "Q": 5, "Z": 3}
+NB_ON_GPSIMD = (2, 5)
+STORES = [(0, 1), (2, 3), (4, 5), (6, 6), (7, 7)]
+
+
+def load_order():
+    items = [("W", 0)]
+    for r in range(ROUNDS):
+        items.append(("X", r))
+        items.append(("Q", r))
+        for h in Z_OF_ROUND.get(r, []):
+            items.append(("Z", h))
+    for h in Z_OF_ROUND.get(ROUNDS, []) + Z_TAIL:
+        items.append(("Z", h))
+    return items
 
 
 def tile_proto_metric_semi_kernel(tc, x1, x2, x3, w, out):
     nc = tc.nc
     q_dram = x1.rearrange("(p t) d a b -> p t (d a b)", t=16)
     x3_dram = x3.rearrange("(c p j) d -> c p j d", p=P, j=4)
-    x2_dram = x2.flatten_outer_dims().rearrange("(h p s) d -> h p s d", p=P, s=4)
+    x2_dram = x2.flatten_outer_dims().rearrange("(h p s) d -> h p s d", p=P, s=2)
     w_dram = w.rearrange("(c p j) m -> p c j m", p=P, j=4)
     out_dram = out.rearrange("(p t) j -> p t j", t=16)
 
@@ -79,11 +52,43 @@ def tile_proto_metric_semi_kernel(tc, x1, x2, x3, w, out):
         psum = ctx.enter_context(tc.psum_pool(name="psum", bufs=1))
         ctx.enter_context(tc.manual_schedule())
 
+        items = load_order()
+        held = {"W": 0, "X": 0, "Q": 0, "Z": 0}
+        raw = {}
+        state = {"pos": 0}
+
+        def load_ahead():
+            while state["pos"] < len(items):
+                kind, i = items[state["pos"]]
+                if held[kind] >= DEPTH[kind]:
+                    break
+                if kind == "W":
+                    t = keep.tile([P, 8, 4, C], BF16, name="w_sb", tag="big0")
+                    nc.sync.dma_start(out=t, in_=w_dram)
+                elif kind == "X":
+                    t = stream.tile([P, 4, D], BF16, name="x3raw", tag="x3raw", bufs=DEPTH["X"])
+                    nc.sync.dma_start(out=t, in_=x3_dram[i])
+                elif kind == "Z":
+                    t = stream.tile([P, 2, D], BF16, name="x2raw", tag="x2raw", bufs=DEPTH["Z"])
+                    nc.sync.dma_start(out=t, in_=x2_dram[i])
+                else:
+                    t = stream.tile([P, 2 * D], BF16, name="qraw", tag="qraw", bufs=DEPTH["Q"])
+                    nc.sync.dma_start(out=t.rearrange("p (t d) -> p t d", t=2), in_=q_dram[:, 2 * i:2 * i + 2, :])
+                raw[(kind, i)] = t
+                held[kind] += 1
+                state["pos"] += 1
+
+        def release(kind):
+            held[kind] -= 1
+            load_ahead()
+
+        load_ahead()
+
         ident = const.tile([P, P], F32, name="ident")
         make_identity(nc, ident)
-        sel_f = const.tile([P, 32], F32, name="sel_f")
-        nc.vector.tensor_reduce(out=sel_f, in_=ident.rearrange("p (n i) -> p n i", i=4), axis=AX.X, op=ALU.add)
-        sel = const.tile([P, 32], BF16, name="sel")
+        sel_f = const.tile([P, 16], F32, name="sel_f")
+        nc.vector.tensor_reduce(out=sel_f, in_=ident.rearrange("p (n i) -> p n i", i=8), axis=AX.X, op=ALU.add)
+        sel = const.tile([P, 16], BF16, name="sel")
         nc.vector.tensor_copy(out=sel, in_=sel_f)
         ones = const.tile([P, 2], BF16, name="ones")
         nc.vector.memset(ones, 1.0)
@@ -92,203 +97,206 @@ def tile_proto_metric_semi_kernel(tc, x1, x2, x3, w, out):
         q_scales = keep.tile([P, 3, B], U8, name="q_scales", align_bytes=64)
         q2 = keep.tile([P, 16], F32, name="q2")
         junk = keep.tile([P, D], BF16, name="junk")
+        nb = keep.tile([P, 16, C], F32, name="nb")
         o_sb = keep.tile([P, 16, C], F32, name="o_sb")
         w_codes = keep.tile([P, 8 * C], U32, name="w_codes", align_bytes=64)
         w_scales = keep.tile([P, 8 * C], U8, name="w_scales", align_bytes=64)
-
         T = {}
-        cr_tags = ["a1", "a2", "b0", "b1"]
 
-        def copier(eng):
-            return nc.vector.tensor_copy if eng == "V" else nc.scalar.copy
+        w_sb = raw[("W", 0)]
+        w_g = keep.tile([P, 8, C, 4], BF16, name="w_g", tag="big1", align_bytes=64)
+        nc.vector.tensor_copy(out=w_g[:, 0:4], in_=w_sb[:, 0:4].rearrange("p c j m -> p c m j"))
+        nc.scalar.copy(out=w_g[:, 4:8], in_=w_sb[:, 4:8].rearrange("p c j m -> p c m j"))
+        for h in range(2):
+            nc.vector.quantize_mx(out=w_codes[:, 512 * h:512 * h + 512].bitcast(FP8X4),
+                                  scales=w_scales[:, 512 * h:512 * h + 512],
+                                  in_=w_g[:, 4 * h:4 * h + 4].rearrange("p c m j -> p (c m j)"))
+        den_ps = psum.tile([P, 512], F32, name="den_ps", tag="zp", bufs=2)
+        for c in range(8):
+            for j in range(4):
+                nc.tensor.matmul(out=den_ps[:, 0:2], lhsT=w_sb[:, c, j, :], rhs=ones,
+                                 start=(c == 0 and j == 0), stop=(c == 7 and j == 3))
+        den = const.tile([P, 1], F32, name="den")
+        nc.vector.tensor_scalar_add(out=den, in0=den_ps[:, 0:1], scalar1=float(SHOT))
+        rden = const.tile([P, 1], F32, name="rden")
+        nc.vector.reciprocal(out=rden, in_=den)
 
-        for tok in ORDER:
-            op = tok[0]
-            if op == "LD":
-                kind, i = tok[1], tok[2]
-                if kind == "W":
-                    t = keep.tile([P, 8, 4, C], BF16, name="w_sb", tag="big0")
-                    nc.sync.dma_start(out=t, in_=w_dram)
-                elif kind == "X":
-                    t = stream.tile([P, 4, D], BF16, name="x3raw", tag="x3raw", bufs=3)
-                    nc.sync.dma_start(out=t, in_=x3_dram[i])
-                elif kind == "Z":
-                    t = stream.tile([P, 4, D], BF16, name="x2raw", tag="x2raw", bufs=2)
-                    nc.sync.dma_start(out=t, in_=x2_dram[i])
-                else:
-                    t = stream.tile([P, 2 * D], BF16, name="qraw", tag="qraw", bufs=5)
-                    nc.sync.dma_start(out=t.rearrange("p (t d) -> p t d", t=2), in_=q_dram[:, 2 * i:2 * i + 2, :])
-                T[(kind, i)] = t
-            elif op == "WR":
-                h = tok[1]
-                if "w_g" not in T:
-                    T["w_g"] = keep.tile([P, 8, C, 4], BF16, name="w_g", tag="big1", align_bytes=64)
-                copier(tok[2])(out=T["w_g"][:, 4 * h:4 * h + 4],
-                               in_=T[("W", 0)][:, 4 * h:4 * h + 4].rearrange("p c j m -> p c m j"))
-            elif op == "WQ":
-                h = tok[1]
-                nc.vector.quantize_mx(out=w_codes[:, 512 * h:512 * h + 512].bitcast(FP8X4),
-                                      scales=w_scales[:, 512 * h:512 * h + 512],
-                                      in_=T["w_g"][:, 4 * h:4 * h + 4].rearrange("p c m j -> p (c m j)"))
-            elif op == "DEN":
-                T["den_ps"] = psum.tile([P, 2], F32, name="den_ps", tag="b0")
-                for c in range(8):
-                    for j in range(4):
-                        nc.tensor.matmul(out=T["den_ps"], lhsT=T[("W", 0)][:, c, j, :], rhs=ones,
-                                         start=(c == 0 and j == 0), stop=(c == 7 and j == 3))
-            elif op == "DENV":
-                den = const.tile([P, 1], F32, name="den")
-                nc.vector.tensor_scalar_add(out=den, in0=T["den_ps"][:, 0:1], scalar1=float(SHOT))
-                T["rden"] = const.tile([P, 1], F32, name="rden")
-                nc.vector.reciprocal(out=T["rden"], in_=den)
-            elif op == "XR":
-                c, lo, hi = tok[1], tok[2], tok[3]
-                if ("g", c) not in T:
-                    T[("g", c)] = stream.tile([P, D, 4], BF16, name="x3g", tag="x3g", bufs=2, align_bytes=64)
-                copier(tok[4])(out=T[("g", c)][:, lo:hi, :].rearrange("p (c i) t -> p c t i", i=4),
-                               in_=T[("X", c)][:, :, lo:hi].rearrange("p t (c i) -> p c t i", i=4))
-            elif op == "XQ":
-                c, n = tok[1], tok[2]
-                if ("c", c) not in T:
-                    T[("c", c)] = stream.tile([P, D], U32, name="x3c", tag="x3c", bufs=2, align_bytes=64)
-                    T[("s", c)] = stream.tile([P, D], U8, name="x3s", tag="x3s", bufs=2, align_bytes=64)
+        def regroup(copy, dst, src, lo, hi):
+            copy(out=dst[:, lo:hi, :].rearrange("p (c i) t -> p c t i", i=4),
+                 in_=src[:, :, lo:hi].rearrange("p t (c i) -> p c t i", i=4))
+
+        def x_regroup(c):
+            g = stream.tile([P, D, 4], BF16, name="x3g", tag="x3g", bufs=2, align_bytes=64)
+            T[("g", c)] = g
+            regroup(nc.vector.tensor_copy, g, raw[("X", c)], 0, D - S_COLS)
+            regroup(nc.scalar.copy, g, raw[("X", c)], D - S_COLS, D)
+            release("X")
+
+        def x_quantise(c):
+            codes = stream.tile([P, D], U32, name="x3c", tag="x3c", bufs=2, align_bytes=64)
+            scales = stream.tile([P, D], U8, name="x3s", tag="x3s", bufs=2, align_bytes=64)
+            T[("c", c)] = codes
+            T[("s", c)] = scales
+            for n in range(3):
                 cols = slice(512 * n, 512 * n + 512)
-                nc.vector.quantize_mx(out=T[("c", c)][:, cols].bitcast(FP8X4), scales=T[("s", c)][:, cols],
+                nc.vector.quantize_mx(out=codes[:, cols].bitcast(FP8X4), scales=scales[:, cols],
                                       in_=T[("g", c)][:, cols, :].rearrange("p c t -> p (c t)"))
-            elif op == "XM":
-                c, n = tok[1], tok[2]
-                if ("wu", n) not in T:
+
+        def x_matmul(c):
+            for n in range(3):
+                if c == 0:
                     T[("wu", n)] = psum.tile([P, 512], F32, name="wu%d" % n, tag="a%d" % n)
                 cols = slice(512 * n, 512 * n + 512)
                 nc.tensor.matmul_mx(out=T[("wu", n)], lhsT=w_codes[:, C * c:C * c + C].bitcast(FP8X4),
                                     lhsT_scale=w_scales[:, C * c:C * c + C],
                                     rhs=T[("c", c)][:, cols].bitcast(FP8X4), rhs_scale=T[("s", c)][:, cols],
                                     start=(c == 0), stop=(c == 7))
-            elif op == "ZM":
-                h, b = tok[1], tok[2]
-                if ("st", b) not in T:
-                    T[("st", b)] = psum.tile([P, 4, C], F32, name="st%d" % b, tag="b%d" % b)
-                for i in range(4):
-                    for s in range(4):
-                        lo = P * (4 * b + i)
-                        nc.tensor.matmul(out=T[("st", b)][:, i, 32 * h:32 * h + 32],
-                                         lhsT=T[("Z", h)][:, s, lo:lo + P], rhs=sel,
-                                         start=(s == 0), stop=(s == 3))
-            elif op == "SE":
-                b = tok[1]
-                if "st_sb" not in T:
-                    T["st_sb"] = keep.tile([P, 12, C], F32, name="st_sb", tag="big0")
-                copier(tok[2])(out=T["st_sb"][:, 4 * b:4 * b + 4, :], in_=T[("st", b)])
-            elif op == "STT":
-                b = tok[1]
-                T[("s_ps", b)] = psum.tile([P, 512], F32, name="s_ps%d" % b, tag="b%d" % b)
-                for i in range(4):
-                    nc.tensor.transpose(out=T[("s_ps", b)][:, P * i:P * i + P], in_=T["st_sb"][:, 4 * b + i, :],
-                                        identity=ident)
-            elif op == "SS":
-                b = tok[1]
-                if "ssc" not in T:
-                    T["ssc"] = keep.tile([P, D], F32, name="ssc", tag="big1", align_bytes=64)
-                cols = slice(512 * b, 512 * b + 512)
-                if tok[2] == "V":
-                    nc.vector.tensor_scalar_mul(out=T["ssc"][:, cols], in0=T[("s_ps", b)], scalar1=T["rden"][:, 0:1])
-                else:
-                    nc.scalar.activation(out=T["ssc"][:, cols], in_=T[("s_ps", b)], func=ACT.Copy,
-                                         scale=T["rden"][:, 0:1])
-            elif op == "PR":
-                n = tok[1]
-                if "proto" not in T:
-                    T["proto"] = keep.tile([P, D], F32, name="proto")
-                cols = slice(512 * n, 512 * n + 512)
-                nc.vector.scalar_tensor_tensor(out=T["proto"][:, cols], in0=T[("wu", n)], scalar=T["rden"][:, 0:1],
-                                               in1=T["ssc"][:, cols], op0=ALU.mult, op1=ALU.add)
-            elif op == "PT":
-                g = tok[1]
-                pview = T["proto"].rearrange("j (g u p e) -> j g u e p", g=3, u=2, p=P, e=2)
-                T[("pt", g)] = psum.tile([P, 4, C], F32, name="pt%d" % g, tag="b%d" % g)
-                for u in range(2):
-                    for e in range(2):
-                        nc.tensor.transpose(out=T[("pt", g)][:, 2 * u + e, :], in_=pview[:, g, u, e, :], identity=ident)
-            elif op == "PC":
-                g = tok[1]
-                if "pg" not in T:
-                    T["pg"] = keep.tile([P, 3, C, 4], BF16, name="pg", align_bytes=64)
-                copier(tok[2])(out=T["pg"][:, g], in_=T[("pt", g)].rearrange("p t j -> p j t"))
-            elif op == "PQ":
-                g = tok[1]
-                if "p_codes" not in T:
-                    T["p_codes"] = keep.tile([P, 3, C], U32, name="p_codes", align_bytes=64)
-                    T["p_scales"] = keep.tile([P, 3, C], U8, name="p_scales", align_bytes=64)
-                nc.vector.quantize_mx(out=T["p_codes"][:, g, :].bitcast(FP8X4), scales=T["p_scales"][:, g, :],
-                                      in_=T["pg"][:, g].rearrange("p j t -> p (j t)"))
-            elif op == "P2":
-                n = tok[1]
-                if "p2parts" not in T:
-                    T["p2parts"] = const.tile([P, 3], F32, name="p2parts")
-                cols = slice(512 * n, 512 * n + 512)
-                nc.scalar.activation(out=junk[:, cols], in_=T["proto"][:, cols], func=ACT.Square,
-                                     accum_out=T["p2parts"][:, n:n + 1])
-            elif op == "P2R":
-                T["p2"] = const.tile([P, 1], F32, name="p2")
-                nc.vector.tensor_reduce(out=T["p2"], in_=T["p2parts"], axis=AX.X, op=ALU.add)
-            elif op == "P2M":
-                T["p2b_ps"] = psum.tile([P, C], F32, name="p2b_ps", tag="a0")
-                nc.tensor.matmul(out=T["p2b_ps"], lhsT=T["p2"][:, 0:1].to_broadcast([P, P]), rhs=ident,
-                                 start=True, stop=True)
-            elif op == "P2C":
-                T["p2b"] = keep.tile([P, C], F32, name="p2b")
-                nc.scalar.copy(out=T["p2b"], in_=T["p2b_ps"])
-            elif op == "QT":
-                k, g = tok[1], tok[2]
-                words = T[("Q", k)].bitcast(F32)
-                xt = psum.tile([P, 2, 2, P], F32, name="xt", tag="xt", bufs=2)
+
+        def q_squares(k):
+            for tt in range(2):
+                nc.scalar.activation(out=junk, in_=raw[("Q", k)][:, D * tt:D * tt + D], func=ACT.Square,
+                                     accum_out=q2[:, 2 * k + tt:2 * k + tt + 1])
+
+        def q_transpose(k):
+            words = raw[("Q", k)].bitcast(F32)
+            for g in range(3):
+                xt = psum.tile([P, 2, 2, P], F32, name="xt", tag="xt", bufs=3)
                 T[("xt", k, g)] = xt
                 for tt in range(2):
                     for u in range(2):
                         lo = 768 * tt + 256 * g + 128 * u
                         nc.tensor.transpose(out=xt[:, tt, u, :], in_=words[:, lo:lo + 128], identity=ident)
-            elif op == "QE":
-                k, g = tok[1], tok[2]
-                if ("qg", k) not in T:
-                    T[("qg", k)] = stream.tile([P, 3 * 256 * 4], BF16, name="qg", tag="qg", bufs=2, align_bytes=64)
-                qg_w = T[("qg", k)].bitcast(F32)
-                copier(tok[3])(out=qg_w[:, 512 * g:512 * g + 512].rearrange("p (t i u) -> p t i u", t=2, u=2),
+
+        def q_copy_out(k):
+            qg = stream.tile([P, 3 * 256 * 4], BF16, name="qg", tag="qg", bufs=2, align_bytes=64)
+            T[("qg", k)] = qg
+            qg_w = qg.bitcast(F32)
+            for g in range(3):
+                nc.scalar.copy(out=qg_w[:, 512 * g:512 * g + 512].rearrange("p (t i u) -> p t i u", t=2, u=2),
                                in_=T[("xt", k, g)].rearrange("p t u i -> p t i u"))
-            elif op == "QS":
-                k, tt = tok[1], tok[2]
-                nc.scalar.activation(out=junk, in_=T[("Q", k)][:, D * tt:D * tt + D], func=ACT.Square,
-                                     accum_out=q2[:, 2 * k + tt:2 * k + tt + 1])
-            elif op == "QQ":
-                k, g = tok[1], tok[2]
+
+        def q_quantise(k):
+            for g in range(3):
                 nc.vector.quantize_mx(out=q_codes[:, g, 256 * k:256 * k + 256].bitcast(FP8X4),
                                       scales=q_scales[:, g, 256 * k:256 * k + 256],
                                       in_=T[("qg", k)][:, 1024 * g:1024 * g + 1024])
-            elif op == "NB":
-                k = tok[1]
-                T[("nb", k)] = stream.tile([P, 2, C], F32, name="nb", tag="nb", bufs=8)
-                eng = nc.vector if tok[2] == "V" else nc.gpsimd
-                eng.tensor_tensor(out=T[("nb", k)], in0=T["p2b"].unsqueeze(1).to_broadcast([P, 2, C]),
-                                  in1=q2[:, 2 * k:2 * k + 2].unsqueeze(2).to_broadcast([P, 2, C]), op=ALU.add)
-            elif op == "CR":
-                k = tok[1]
-                cr = psum.tile([P, 2, C], F32, name="cr", tag=cr_tags[k % 4])
-                T[("cr", k)] = cr
-                for tt in range(2):
-                    cols = slice(P * (2 * k + tt), P * (2 * k + tt) + P)
-                    for g in range(3):
-                        nc.tensor.matmul_mx(out=cr[:, tt, :], lhsT=q_codes[:, g, cols].bitcast(FP8X4),
-                                            lhsT_scale=q_scales[:, g, cols],
-                                            rhs=T["p_codes"][:, g, :].bitcast(FP8X4),
-                                            rhs_scale=T["p_scales"][:, g, :],
-                                            start=(g == 0), stop=(g == 2))
-            elif op == "EP":
-                k = tok[1]
-                nc.vector.scalar_tensor_tensor(out=o_sb[:, 2 * k:2 * k + 2, :].rearrange("p t j -> p (t j)"),
-                                               in0=T[("cr", k)].rearrange("p t j -> p (t j)"), scalar=2.0,
-                                               in1=T[("nb", k)].rearrange("p t j -> p (t j)"),
-                                               op0=ALU.mult, op1=ALU.subtract)
-            elif op == "OUT":
-                k = tok[1]
-                nc.sync.dma_start(out=out_dram[:, 2 * k - 2:2 * k + 2, :], in_=o_sb[:, 2 * k - 2:2 * k + 2, :])
+
+        def z_sum(h):
+            zp = psum.tile([P, 512], F32, name="zp", tag="zp", bufs=2)
+            zv = zp[:, 0:192].rearrange("p (t n) -> p t n", n=16)
+            T[("zv", h)] = zv
+            for dt in range(12):
+                for s in range(2):
+                    nc.tensor.matmul(out=zv[:, dt, :], lhsT=raw[("Z", h)][:, s, P * dt:P * dt + P], rhs=sel,
+                                     start=(s == 0), stop=(s == 1))
+            release("Z")
+
+        def z_copy_out(h):
+            if "st_sb" not in T:
+                T["st_sb"] = keep.tile([P, 12, C], F32, name="st_sb", tag="big0")
+            nc.scalar.copy(out=T["st_sb"][:, :, 16 * h:16 * h + 16], in_=T[("zv", h)])
+
+        def wu_scaled(n):
+            if "wusc" not in T:
+                T["wusc"] = keep.tile([P, D], F32, name="wusc", tag="big1", align_bytes=64)
+            nc.scalar.activation(out=T["wusc"][:, 512 * n:512 * n + 512], in_=T[("wu", n)], func=ACT.Copy,
+                                 scale=rden[:, 0:1])
+
+        for r in range(ROUNDS + 1):
+            if r < ROUNDS:
+                x_regroup(r)
+                q_squares(r)
+                q_transpose(r)
+                release("Q")
+                q_copy_out(r)
+            if r >= 1:
+                q_quantise(r - 1)
+            if r < ROUNDS:
+                x_quantise(r)
+            for h in Z_OF_ROUND.get(r, []):
+                z_sum(h)
+                z_copy_out(h)
+            if r >= 1:
+                x_matmul(r - 1)
+
+        wu_scaled(0)
+        wu_scaled(1)
+        z_sum(Z_TAIL[0])
+        z_copy_out(Z_TAIL[0])
+        wu_scaled(2)
+        z_sum(Z_TAIL[1])
+        z_copy_out(Z_TAIL[1])
+
+        s_ps = []
+        for b in range(3):
+            t = psum.tile([P, 512], F32, name="s_ps%d" % b, tag="a%d" % b)
+            s_ps.append(t)
+            for i in range(4):
+                nc.tensor.transpose(out=t[:, P * i:P * i + P], in_=T["st_sb"][:, 4 * b + i, :], identity=ident)
+        proto = keep.tile([P, 3, 2, 2 * P], F32, name="proto")
+        for b in range(3):
+            nc.vector.scalar_tensor_tensor(
+                out=proto[:, b].rearrange("j e v -> j v e"),
+                in0=s_ps[b].rearrange("j (v e) -> j v e", e=2), scalar=rden[:, 0:1],
+                in1=T["wusc"][:, 512 * b:512 * b + 512].rearrange("j (v e) -> j v e", e=2),
+                op0=ALU.mult, op1=ALU.add)
+        pt = []
+        for g in range(3):
+            t = psum.tile([P, 4, C], F32, name="pt%d" % g, tag="a%d" % g)
+            pt.append(t)
+            for u in range(2):
+                for e in range(2):
+                    nc.tensor.transpose(out=t[:, 2 * u + e, :], in_=proto[:, g, e, P * u:P * u + P], identity=ident)
+        p2parts = const.tile([P, 3], F32, name="p2parts")
+        for b in range(3):
+            nc.scalar.activation(out=junk[:, 0:512], in_=proto[:, b].rearrange("j e v -> j (e v)"), func=ACT.Square,
+                                 accum_out=p2parts[:, b:b + 1])
+        pg = keep.tile([P, 3, C, 4], BF16, name="pg", align_bytes=64)
+        p_codes = keep.tile([P, 3, C], U32, name="p_codes", align_bytes=64)
+        p_scales = keep.tile([P, 3, C], U8, name="p_scales", align_bytes=64)
+
+        def p_copy_out(copy, g):
+            copy(out=pg[:, g], in_=pt[g].rearrange("p t j -> p j t"))
+
+        def p_quantise(g):
+            nc.vector.quantize_mx(out=p_codes[:, g, :].bitcast(FP8X4), scales=p_scales[:, g, :],
+                                  in_=pg[:, g].rearrange("p j t -> p (j t)"))
+
+        p_copy_out(nc.vector.tensor_copy, 0)
+        p_quantise(0)
+        p_copy_out(nc.vector.tensor_copy, 2)
+        p_copy_out(nc.scalar.copy, 1)
+        p2 = const.tile([P, 1], F32, name="p2")
+        nc.vector.tensor_reduce(out=p2, in_=p2parts, axis=AX.X, op=ALU.add)
+        p_quantise(1)
+        p_quantise(2)
+        p2b_ps = psum.tile([P, 512], F32, name="p2b_ps", tag="a0")
+        nc.tensor.matmul(out=p2b_ps[:, 0:C], lhsT=p2[:, 0:1].to_broadcast([P, P]), rhs=ident, start=True, stop=True)
+        p2b = keep.tile([P, C], F32, name="p2b")
+        nc.scalar.copy(out=p2b, in_=p2b_ps[:, 0:C])
+
+        for k in range(8):
+            if k in NB_ON_GPSIMD:
+                nc.gpsimd.tensor_tensor(out=nb[:, 2 * k:2 * k + 2, :], in0=p2b.unsqueeze(1).to_broadcast([P, 2, C]),
+                                        in1=q2[:, 2 * k:2 * k + 2].unsqueeze(2).to_broadcast([P, 2, C]), op=ALU.add)
             else:
-                assert False, op
+                for t in (2 * k, 2 * k + 1):
+                    nc.scalar.activation(out=nb[:, t, :], in_=p2b, func=ACT.Identity, bias=q2[:, t:t + 1], scale=1.0)
+            if k % 5 < 3:
+                bank = psum.tile([P, 512], F32, name="cr", tag="xt", bufs=3)
+            else:
+                bank = psum.tile([P, 512], F32, name="cr", tag="zp", bufs=2)
+            for tt in range(2):
+                cols = slice(P * (2 * k + tt), P * (2 * k + tt) + P)
+                for g in range(3):
+                    nc.tensor.matmul_mx(out=bank[:, C * tt:C * tt + C], lhsT=q_codes[:, g, cols].bitcast(FP8X4),
+                                        lhsT_scale=q_scales[:, g, cols],
+                                        rhs=p_codes[:, g, :].bitcast(FP8X4), rhs_scale=p_scales[:, g, :],
+                                        start=(g == 0), stop=(g == 2))
+            nc.vector.scalar_tensor_tensor(out=o_sb[:, 2 * k:2 * k + 2, :].rearrange("p t j -> p (t j)"),
+                                           in0=bank[:, 0:2 * C], scalar=2.0,
+                                           in1=nb[:, 2 * k:2 * k + 2, :].rearrange("p t j -> p (t j)"),
+                                           op0=ALU.mult, op1=ALU.subtract)
+            for first, last in STORES:
+                if last == k:
+                    nc.sync.dma_start(out=out_dram[:, 2 * first:2 * last + 2, :], in_=o_sb[:, 2 * first:2 * last + 2, :])

@@ -21,7 +21,6 @@ S_COLS = 64
 Z_OF_ROUND = {3: [0], 4: [1], 5: [2], 6: [3], 7: [4], 8: [5]}
 Z_TAIL = [6, 7]
 DEPTH = {"W": 1, "X": 3, "Q": 5, "Z": 3}
-NB_ON_GPSIMD = (2, 5)
 STORES = [(0, 1), (2, 3), (4, 5), (6, 6), (7, 7)]
 
 
@@ -70,7 +69,11 @@ def tile_proto_metric_semi_kernel(tc, x1, x2, x3, w, out):
                     nc.sync.dma_start(out=t, in_=x3_dram[i])
                 elif kind == "Z":
                     t = stream.tile([P, 2, D], BF16, name="x2raw", tag="x2raw", bufs=DEPTH["Z"])
-                    nc.sync.dma_start(out=t, in_=x2_dram[i])
+                    if i == Z_TAIL[-1]:
+                        nc.sync.dma_start(out=t[:, :, 0:D // 2], in_=x2_dram[i][:, :, 0:D // 2])
+                        nc.sync.dma_start(out=t[:, :, D // 2:D], in_=x2_dram[i][:, :, D // 2:D])
+                    else:
+                        nc.sync.dma_start(out=t, in_=x2_dram[i])
                 else:
                     t = stream.tile([P, 2 * D], BF16, name="qraw", tag="qraw", bufs=DEPTH["Q"])
                     nc.sync.dma_start(out=t.rearrange("p (t d) -> p t d", t=2), in_=q_dram[:, 2 * i:2 * i + 2, :])
@@ -97,7 +100,6 @@ def tile_proto_metric_semi_kernel(tc, x1, x2, x3, w, out):
         q_scales = keep.tile([P, 3, B], U8, name="q_scales", align_bytes=64)
         q2 = keep.tile([P, 16], F32, name="q2")
         junk = keep.tile([P, D], BF16, name="junk")
-        nb = keep.tile([P, 16, C], F32, name="nb")
         o_sb = keep.tile([P, 16, C], F32, name="o_sb")
         w_codes = keep.tile([P, 8 * C], U32, name="w_codes", align_bytes=64)
         w_scales = keep.tile([P, 8 * C], U8, name="w_scales", align_bytes=64)
@@ -117,7 +119,7 @@ def tile_proto_metric_semi_kernel(tc, x1, x2, x3, w, out):
                 nc.tensor.matmul(out=den_ps[:, 0:2], lhsT=w_sb[:, c, j, :], rhs=ones,
                                  start=(c == 0 and j == 0), stop=(c == 7 and j == 3))
         den = const.tile([P, 1], F32, name="den")
-        nc.vector.tensor_scalar_add(out=den, in0=den_ps[:, 0:1], scalar1=float(SHOT))
+        nc.vector.tensor_scalar(out=den, in0=den_ps[:, 0:1], scalar1=float(SHOT), scalar2=0.5, op0=ALU.add, op1=ALU.mult)
         rden = const.tile([P, 1], F32, name="rden")
         nc.vector.reciprocal(out=rden, in_=den)
 
@@ -250,7 +252,7 @@ def tile_proto_metric_semi_kernel(tc, x1, x2, x3, w, out):
         p2parts = const.tile([P, 3], F32, name="p2parts")
         for b in range(3):
             nc.scalar.activation(out=junk[:, 0:512], in_=proto[:, b].rearrange("j e v -> j (e v)"), func=ACT.Square,
-                                 accum_out=p2parts[:, b:b + 1])
+                                 scale=0.5, accum_out=p2parts[:, b:b + 1])
         pg = keep.tile([P, 3, C, 4], BF16, name="pg", align_bytes=64)
         p_codes = keep.tile([P, 3, C], U32, name="p_codes", align_bytes=64)
         p_scales = keep.tile([P, 3, C], U8, name="p_scales", align_bytes=64)
@@ -276,12 +278,6 @@ def tile_proto_metric_semi_kernel(tc, x1, x2, x3, w, out):
         nc.scalar.copy(out=p2b, in_=p2b_ps[:, 0:C])
 
         for k in range(8):
-            if k in NB_ON_GPSIMD:
-                nc.gpsimd.tensor_tensor(out=nb[:, 2 * k:2 * k + 2, :], in0=p2b.unsqueeze(1).to_broadcast([P, 2, C]),
-                                        in1=q2[:, 2 * k:2 * k + 2].unsqueeze(2).to_broadcast([P, 2, C]), op=ALU.add)
-            else:
-                for t in (2 * k, 2 * k + 1):
-                    nc.scalar.activation(out=nb[:, t, :], in_=p2b, func=ACT.Identity, bias=q2[:, t:t + 1], scale=1.0)
             if k % 5 < 3:
                 bank = psum.tile([P, 512], F32, name="cr", tag="xt", bufs=3)
             else:
@@ -293,10 +289,10 @@ def tile_proto_metric_semi_kernel(tc, x1, x2, x3, w, out):
                                         lhsT_scale=q_scales[:, g, cols],
                                         rhs=p_codes[:, g, :].bitcast(FP8X4), rhs_scale=p_scales[:, g, :],
                                         start=(g == 0), stop=(g == 2))
-            nc.vector.scalar_tensor_tensor(out=o_sb[:, 2 * k:2 * k + 2, :].rearrange("p t j -> p (t j)"),
-                                           in0=bank[:, 0:2 * C], scalar=2.0,
-                                           in1=nb[:, 2 * k:2 * k + 2, :].rearrange("p t j -> p (t j)"),
-                                           op0=ALU.mult, op1=ALU.subtract)
+            for tt in range(2):
+                nc.vector.scalar_tensor_tensor(out=o_sb[:, 2 * k + tt, :], in0=bank[:, C * tt:C * tt + C],
+                                               scalar=q2[:, 2 * k + tt:2 * k + tt + 1], in1=p2b,
+                                               op0=ALU.subtract, op1=ALU.subtract)
             for first, last in STORES:
                 if last == k:
                     nc.sync.dma_start(out=out_dram[:, 2 * first:2 * last + 2, :], in_=o_sb[:, 2 * first:2 * last + 2, :])

@@ -21,7 +21,11 @@ S_COLS = 64
 Z_OF_ROUND = {3: [0], 4: [1], 5: [2], 6: [3], 7: [4], 8: [5]}
 Z_TAIL = [6, 7]
 DEPTH = {"W": 1, "X": 3, "Q": 5, "Z": 3}
-STORES = [(0, 1), (2, 3), (4, 5), (6, 6), (7, 7)]
+FIRST = 5
+FIRST_TAGS = ["xt", "xt", "xt", "zp", "zp"]
+LATER_TAGS = ["a1", "a2", "xt", "xt", "xt", "zp"]
+TAG_BUFS = {"xt": 3, "zp": 2, "a1": 1, "a2": 1}
+STORES = [(0, 4), (5, 8), (9, 12), (13, 14), (15, 15)]
 
 
 def load_order():
@@ -96,8 +100,8 @@ def tile_proto_metric_semi_kernel(tc, x1, x2, x3, w, out):
         ones = const.tile([P, 2], BF16, name="ones")
         nc.vector.memset(ones, 1.0)
 
-        q_codes = keep.tile([P, 3, B], U32, name="q_codes", align_bytes=64)
-        q_scales = keep.tile([P, 3, B], U8, name="q_scales", align_bytes=64)
+        q_codes = keep.tile([P, 8, 3 * 256], U32, name="q_codes", align_bytes=64)
+        q_scales = keep.tile([P, 8, 3 * 256], U8, name="q_scales", align_bytes=64)
         q2 = keep.tile([P, 16], F32, name="q2")
         junk = keep.tile([P, D], BF16, name="junk")
         o_sb = keep.tile([P, 16, C], F32, name="o_sb")
@@ -139,8 +143,7 @@ def tile_proto_metric_semi_kernel(tc, x1, x2, x3, w, out):
             scales = stream.tile([P, D], U8, name="x3s", tag="x3s", bufs=2, align_bytes=64)
             T[("c", c)] = codes
             T[("s", c)] = scales
-            for n in range(3):
-                cols = slice(512 * n, 512 * n + 512)
+            for cols in (slice(0, 1024), slice(1024, 1536)):
                 nc.vector.quantize_mx(out=codes[:, cols].bitcast(FP8X4), scales=scales[:, cols],
                                       in_=T[("g", c)][:, cols, :].rearrange("p c t -> p (c t)"))
 
@@ -178,10 +181,9 @@ def tile_proto_metric_semi_kernel(tc, x1, x2, x3, w, out):
                                in_=T[("xt", k, g)].rearrange("p t u i -> p t i u"))
 
         def q_quantise(k):
-            for g in range(3):
-                nc.vector.quantize_mx(out=q_codes[:, g, 256 * k:256 * k + 256].bitcast(FP8X4),
-                                      scales=q_scales[:, g, 256 * k:256 * k + 256],
-                                      in_=T[("qg", k)][:, 1024 * g:1024 * g + 1024])
+            for cols in (slice(0, 512), slice(512, 768)):
+                nc.vector.quantize_mx(out=q_codes[:, k, cols].bitcast(FP8X4), scales=q_scales[:, k, cols],
+                                      in_=T[("qg", k)][:, 4 * cols.start:4 * cols.stop])
 
         def z_sum(h):
             zp = psum.tile([P, 512], F32, name="zp", tag="zp", bufs=2)
@@ -264,35 +266,50 @@ def tile_proto_metric_semi_kernel(tc, x1, x2, x3, w, out):
             nc.vector.quantize_mx(out=p_codes[:, g, :].bitcast(FP8X4), scales=p_scales[:, g, :],
                                   in_=pg[:, g].rearrange("p j t -> p (j t)"))
 
+        def cross_pass(dst, t, g):
+            cols = slice(256 * g + P * (t % 2), 256 * g + P * (t % 2) + P)
+            nc.tensor.matmul_mx(out=dst, lhsT=q_codes[:, t // 2, cols].bitcast(FP8X4), lhsT_scale=q_scales[:, t // 2, cols],
+                                rhs=p_codes[:, g, :].bitcast(FP8X4), rhs_scale=p_scales[:, g, :],
+                                start=(g == 0), stop=(g == 2))
+
+        def finish(src, t):
+            nc.vector.scalar_tensor_tensor(out=o_sb[:, t, :], in0=src, scalar=q2[:, t:t + 1], in1=p2b,
+                                           op0=ALU.subtract, op1=ALU.subtract)
+            for first, last in STORES:
+                if last == t:
+                    nc.sync.dma_start(out=out_dram[:, first:last + 1, :], in_=o_sb[:, first:last + 1, :])
+
+        first_banks = []
+        for t in range(FIRST):
+            bank = psum.tile([P, 512], F32, name="cr", tag=FIRST_TAGS[t], bufs=TAG_BUFS[FIRST_TAGS[t]])
+            first_banks.append(bank)
         p_copy_out(nc.vector.tensor_copy, 0)
         p_quantise(0)
-        p_copy_out(nc.vector.tensor_copy, 2)
-        p_copy_out(nc.scalar.copy, 1)
         p2 = const.tile([P, 1], F32, name="p2")
         nc.vector.tensor_reduce(out=p2, in_=p2parts, axis=AX.X, op=ALU.add)
-        p_quantise(1)
-        p_quantise(2)
         p2b_ps = psum.tile([P, 512], F32, name="p2b_ps", tag="a0")
         nc.tensor.matmul(out=p2b_ps[:, 0:C], lhsT=p2[:, 0:1].to_broadcast([P, P]), rhs=ident, start=True, stop=True)
+        for t in range(FIRST):
+            cross_pass(first_banks[t][:, 0:C], t, 0)
+        p_copy_out(nc.vector.tensor_copy, 2)
+        p_copy_out(nc.scalar.copy, 1)
         p2b = keep.tile([P, C], F32, name="p2b")
         nc.scalar.copy(out=p2b, in_=p2b_ps[:, 0:C])
+        p_quantise(1)
+        for t in range(FIRST):
+            cross_pass(first_banks[t][:, 0:C], t, 1)
+        p_quantise(2)
+        for t in range(FIRST):
+            cross_pass(first_banks[t][:, 0:C], t, 2)
 
-        for k in range(8):
-            if k % 5 < 3:
-                bank = psum.tile([P, 512], F32, name="cr", tag="xt", bufs=3)
-            else:
-                bank = psum.tile([P, 512], F32, name="cr", tag="zp", bufs=2)
-            for tt in range(2):
-                cols = slice(P * (2 * k + tt), P * (2 * k + tt) + P)
+        for t in range(FIRST):
+            finish(first_banks[t][:, 0:C], t)
+        for n, t0 in enumerate(range(FIRST, 16, 2)):
+            tag = LATER_TAGS[n]
+            bank = psum.tile([P, 512], F32, name="cr", tag=tag, bufs=TAG_BUFS[tag])
+            pair = [t for t in (t0, t0 + 1) if t < 16]
+            for i, t in enumerate(pair):
                 for g in range(3):
-                    nc.tensor.matmul_mx(out=bank[:, C * tt:C * tt + C], lhsT=q_codes[:, g, cols].bitcast(FP8X4),
-                                        lhsT_scale=q_scales[:, g, cols],
-                                        rhs=p_codes[:, g, :].bitcast(FP8X4), rhs_scale=p_scales[:, g, :],
-                                        start=(g == 0), stop=(g == 2))
-            for tt in range(2):
-                nc.vector.scalar_tensor_tensor(out=o_sb[:, 2 * k + tt, :], in0=bank[:, C * tt:C * tt + C],
-                                               scalar=q2[:, 2 * k + tt:2 * k + tt + 1], in1=p2b,
-                                               op0=ALU.subtract, op1=ALU.subtract)
-            for first, last in STORES:
-                if last == k:
-                    nc.sync.dma_start(out=out_dram[:, 2 * first:2 * last + 2, :], in_=o_sb[:, 2 * first:2 * last + 2, :])
+                    cross_pass(bank[:, C * i:C * i + C], t, g)
+            for i, t in enumerate(pair):
+                finish(bank[:, C * i:C * i + C], t)

@@ -74,8 +74,8 @@ def tile_proto_metric_semi_kernel(tc, x1, x2, x3, w, out):
                 elif kind == "Z":
                     t = stream.tile([P, 2, D], BF16, name="x2raw", tag="x2raw", bufs=DEPTH["Z"])
                     if i == Z_TAIL[-1]:
-                        nc.sync.dma_start(out=t[:, :, 0:D // 2], in_=x2_dram[i][:, :, 0:D // 2])
-                        nc.sync.dma_start(out=t[:, :, D // 2:D], in_=x2_dram[i][:, :, D // 2:D])
+                        for n in range(3):
+                            nc.sync.dma_start(out=t[:, :, 512 * n:512 * n + 512], in_=x2_dram[i][:, :, 512 * n:512 * n + 512])
                     else:
                         nc.sync.dma_start(out=t, in_=x2_dram[i])
                 else:
@@ -200,6 +200,15 @@ def tile_proto_metric_semi_kernel(tc, x1, x2, x3, w, out):
                 T["st_sb"] = keep.tile([P, 12, C], F32, name="st_sb", tag="big0")
             nc.scalar.copy(out=T["st_sb"][:, :, 16 * h:16 * h + 16], in_=T[("zv", h)])
 
+        def z_third(h, n):
+            zp = psum.tile([P, 512], F32, name="zq", tag="xt", bufs=3)
+            zv = zp[:, 0:64].rearrange("p (t n) -> p t n", n=16)
+            for dt in range(4 * n, 4 * n + 4):
+                for s in range(2):
+                    nc.tensor.matmul(out=zv[:, dt - 4 * n, :], lhsT=raw[("Z", h)][:, s, P * dt:P * dt + P], rhs=sel,
+                                     start=(s == 0), stop=(s == 1))
+            nc.scalar.copy(out=T["st_sb"][:, 4 * n:4 * n + 4, 16 * h:16 * h + 16], in_=zv)
+
         def wu_scaled(n):
             if "wusc" not in T:
                 T["wusc"] = keep.tile([P, D], F32, name="wusc", tag="big1", align_bytes=64)
@@ -228,15 +237,20 @@ def tile_proto_metric_semi_kernel(tc, x1, x2, x3, w, out):
         z_sum(Z_TAIL[0])
         z_copy_out(Z_TAIL[0])
         wu_scaled(2)
-        z_sum(Z_TAIL[1])
-        z_copy_out(Z_TAIL[1])
 
         s_ps = []
-        for b in range(3):
+
+        def s_back(b):
             t = psum.tile([P, 512], F32, name="s_ps%d" % b, tag="a%d" % b)
             s_ps.append(t)
             for i in range(4):
                 nc.tensor.transpose(out=t[:, P * i:P * i + P], in_=T["st_sb"][:, 4 * b + i, :], identity=ident)
+
+        for n in range(3):
+            z_third(Z_TAIL[1], n)
+        release("Z")
+        for b in range(3):
+            s_back(b)
         proto = keep.tile([P, 3, 2, 2 * P], F32, name="proto")
         for b in range(3):
             nc.vector.scalar_tensor_tensor(

@@ -19,7 +19,8 @@ FLOPS = 2 * U * C * D + 2 * B * C * D
 ROUNDS = 8
 S_COLS = 64
 Z_OF_ROUND = {3: [0], 4: [1], 5: [2], 6: [3], 7: [4], 8: [5]}
-Z_TAIL = [6, 7]
+Z_TAIL = []
+PAIR_ROW = 6 * 256
 DEPTH = {"W": 1, "X": 3, "Q": 5, "Z": 3}
 FIRST = 5
 FIRST_TAGS = ["xt", "xt", "xt", "zp", "zp"]
@@ -37,6 +38,7 @@ def load_order():
             items.append(("Z", h))
     for h in Z_OF_ROUND.get(ROUNDS, []) + Z_TAIL:
         items.append(("Z", h))
+    items.append(("Y", 0))
     return items
 
 
@@ -46,6 +48,7 @@ def tile_proto_metric_semi_kernel(tc, x1, x2, x3, w, out):
     x3_dram = x3.rearrange("(c p j) d -> c p j d", p=P, j=4)
     x2_dram = x2.flatten_outer_dims().rearrange("(h p s) d -> h p s d", p=P, s=2)
     w_dram = w.rearrange("(c p j) m -> p c j m", p=P, j=4)
+    y_dram = x2.flatten_outer_dims()[PAIR_ROW:PAIR_ROW + 512, :].rearrange("(p s) d -> p s d", s=4)
     out_dram = out.rearrange("(p t) j -> p t j", t=16)
 
     with ExitStack() as ctx:
@@ -63,6 +66,15 @@ def tile_proto_metric_semi_kernel(tc, x1, x2, x3, w, out):
         def load_ahead():
             while state["pos"] < len(items):
                 kind, i = items[state["pos"]]
+                if kind == "Y":
+                    if held["X"] >= DEPTH["X"]:
+                        break
+                    t = stream.tile([P, 4, D], BF16, name="x2pair", tag="x3raw", bufs=DEPTH["X"])
+                    for n in range(3):
+                        nc.sync.dma_start(out=t[:, :, 512 * n:512 * n + 512], in_=y_dram[:, :, 512 * n:512 * n + 512])
+                    raw[(kind, i)] = t
+                    state["pos"] += 1
+                    continue
                 if held[kind] >= DEPTH[kind]:
                     break
                 if kind == "W":
@@ -73,11 +85,7 @@ def tile_proto_metric_semi_kernel(tc, x1, x2, x3, w, out):
                     nc.sync.dma_start(out=t, in_=x3_dram[i])
                 elif kind == "Z":
                     t = stream.tile([P, 2, D], BF16, name="x2raw", tag="x2raw", bufs=DEPTH["Z"])
-                    if i == Z_TAIL[-1]:
-                        for n in range(3):
-                            nc.sync.dma_start(out=t[:, :, 512 * n:512 * n + 512], in_=x2_dram[i][:, :, 512 * n:512 * n + 512])
-                    else:
-                        nc.sync.dma_start(out=t, in_=x2_dram[i])
+                    nc.sync.dma_start(out=t, in_=x2_dram[i])
                 else:
                     t = stream.tile([P, 2 * D], BF16, name="qraw", tag="qraw", bufs=DEPTH["Q"])
                     nc.sync.dma_start(out=t.rearrange("p (t d) -> p t d", t=2), in_=q_dram[:, 2 * i:2 * i + 2, :])
@@ -97,6 +105,10 @@ def tile_proto_metric_semi_kernel(tc, x1, x2, x3, w, out):
         nc.vector.tensor_reduce(out=sel_f, in_=ident.rearrange("p (n i) -> p n i", i=8), axis=AX.X, op=ALU.add)
         sel = const.tile([P, 16], BF16, name="sel")
         nc.vector.tensor_copy(out=sel, in_=sel_f)
+        sel4_f = const.tile([P, 32], F32, name="sel4_f")
+        nc.vector.tensor_reduce(out=sel4_f, in_=ident.rearrange("p (n i) -> p n i", i=4), axis=AX.X, op=ALU.add)
+        sel4 = const.tile([P, 32], BF16, name="sel4")
+        nc.vector.tensor_copy(out=sel4, in_=sel4_f)
         ones = const.tile([P, 2], BF16, name="ones")
         nc.vector.memset(ones, 1.0)
 
@@ -200,14 +212,17 @@ def tile_proto_metric_semi_kernel(tc, x1, x2, x3, w, out):
                 T["st_sb"] = keep.tile([P, 12, C], F32, name="st_sb", tag="big0")
             nc.scalar.copy(out=T["st_sb"][:, :, 16 * h:16 * h + 16], in_=T[("zv", h)])
 
-        def z_third(h, n):
+        def pair_sum(n):
             zp = psum.tile([P, 512], F32, name="zq", tag="xt", bufs=3)
-            zv = zp[:, 0:64].rearrange("p (t n) -> p t n", n=16)
+            zv = zp[:, 0:128].rearrange("p (t n) -> p t n", n=32)
+            T[("yv", n)] = zv
             for dt in range(4 * n, 4 * n + 4):
-                for s in range(2):
-                    nc.tensor.matmul(out=zv[:, dt - 4 * n, :], lhsT=raw[("Z", h)][:, s, P * dt:P * dt + P], rhs=sel,
-                                     start=(s == 0), stop=(s == 1))
-            nc.scalar.copy(out=T["st_sb"][:, 4 * n:4 * n + 4, 16 * h:16 * h + 16], in_=zv)
+                for s in range(4):
+                    nc.tensor.matmul(out=zv[:, dt - 4 * n, :], lhsT=raw[("Y", 0)][:, s, P * dt:P * dt + P], rhs=sel4,
+                                     start=(s == 0), stop=(s == 3))
+
+        def pair_copy_out(n):
+            nc.scalar.copy(out=T["st_sb"][:, 4 * n:4 * n + 4, 96:128], in_=T[("yv", n)])
 
         def wu_scaled(n):
             if "wusc" not in T:
@@ -229,13 +244,16 @@ def tile_proto_metric_semi_kernel(tc, x1, x2, x3, w, out):
             for h in Z_OF_ROUND.get(r, []):
                 z_sum(h)
                 z_copy_out(h)
+            if r == ROUNDS:
+                pair_sum(0)
+                pair_copy_out(0)
             if r >= 1:
                 x_matmul(r - 1)
 
         wu_scaled(0)
         wu_scaled(1)
-        z_sum(Z_TAIL[0])
-        z_copy_out(Z_TAIL[0])
+        pair_sum(1)
+        pair_copy_out(1)
         wu_scaled(2)
 
         s_ps = []
@@ -246,11 +264,11 @@ def tile_proto_metric_semi_kernel(tc, x1, x2, x3, w, out):
             for i in range(4):
                 nc.tensor.transpose(out=t[:, P * i:P * i + P], in_=T["st_sb"][:, 4 * b + i, :], identity=ident)
 
-        for n in range(3):
-            z_third(Z_TAIL[1], n)
-        release("Z")
-        for b in range(3):
-            s_back(b)
+        s_back(0)
+        pair_sum(2)
+        pair_copy_out(2)
+        s_back(1)
+        s_back(2)
         proto = keep.tile([P, 3, 2, 2 * P], F32, name="proto")
         for b in range(3):
             nc.vector.scalar_tensor_tensor(

@@ -284,9 +284,13 @@ def tile_proto_metric_semi_kernel(tc, x1, x2, x3, w, out):
                 for e in range(2):
                     nc.tensor.transpose(out=t[:, 2 * u + e, :], in_=proto[:, g, e, P * u:P * u + P], identity=ident)
         p2parts = const.tile([P, 3], F32, name="p2parts")
+        p2sums = const.tile([P, 2], F32, name="p2sums")
         for b in range(3):
             nc.scalar.activation(out=junk[:, 0:512], in_=proto[:, b].rearrange("j e v -> j (e v)"), func=ACT.Square,
                                  scale=0.5, accum_out=p2parts[:, b:b + 1])
+            if b >= 1:
+                nc.scalar.activation(out=p2sums[:, b - 1:b], in_=p2parts[:, b:b + 1], func=ACT.Identity,
+                                     bias=(p2parts[:, 0:1] if b == 1 else p2sums[:, 0:1]), scale=1.0)
         pg = keep.tile([P, 3, C, 4], BF16, name="pg", align_bytes=64)
         p_codes = keep.tile([P, 3, C], U32, name="p_codes", align_bytes=64)
         p_scales = keep.tile([P, 3, C], U8, name="p_scales", align_bytes=64)
@@ -317,10 +321,8 @@ def tile_proto_metric_semi_kernel(tc, x1, x2, x3, w, out):
             first_banks.append(bank)
         p_copy_out(nc.vector.tensor_copy, 0)
         p_quantise(0)
-        p2 = const.tile([P, 1], F32, name="p2")
-        nc.vector.tensor_reduce(out=p2, in_=p2parts, axis=AX.X, op=ALU.add)
         p2b_ps = psum.tile([P, 512], F32, name="p2b_ps", tag="a0")
-        nc.tensor.matmul(out=p2b_ps[:, 0:C], lhsT=p2[:, 0:1].to_broadcast([P, P]), rhs=ident, start=True, stop=True)
+        nc.tensor.matmul(out=p2b_ps[:, 0:C], lhsT=p2sums[:, 1:2].to_broadcast([P, P]), rhs=ident, start=True, stop=True)
         for t in range(FIRST):
             cross_pass(first_banks[t][:, 0:C], t, 0)
         p_copy_out(nc.vector.tensor_copy, 2)

from contextlib import ExitStack

import concourse.mybir as mybir
from concourse.masks import make_identity

F32 = mybir.dt.float32
BF16 = mybir.dt.bfloat16
U32 = mybir.dt.uint32
U8 = mybir.dt.uint8
FP8X4 = mybir.dt.float8_e4m3fn_x4
ALU = mybir.AluOpType
ACT = mybir.ActivationFunctionType
AX = mybir.AxisListType

P = 128
B, D, C, SHOT, U = 2048, 1536, 128, 16, 4096
FLOPS = 2 * U * C * D + 2 * B * C * D

ROUNDS = 8
S_COLS = 64
Z_OF_ROUND = {3: [0], 4: [1], 5: [2], 6: [3], 7: [4], 8: [5]}
Z_TAIL = []
PAIR_ROW = 6 * 256
DEPTH = {"W": 1, "X": 3, "Q": 5, "Z": 3}
FIRST = 5
FIRST_TAGS = ["xt", "xt", "xt", "zp", "zp"]
LATER_TAGS = ["a1", "a2", "xt", "xt", "xt", "zp"]
TAG_BUFS = {"xt": 3, "zp": 2, "a1": 1, "a2": 1}
STORES = [(0, 4), (5, 8), (9, 12), (13, 14), (15, 15)]


def load_order():
    items = [("W", 0)]
    for r in range(ROUNDS):
        items.append(("X", r))
        items.append(("Q", r))
        for h in Z_OF_ROUND.get(r, []):
            items.append(("Z", h))
    for h in Z_OF_ROUND.get(ROUNDS, []) + Z_TAIL:
        items.append(("Z", h))
    items.append(("Y", 0))
    return items


def tile_proto_metric_semi_kernel(tc, x1, x2, x3, w, out):
    nc = tc.nc
    q_dram = x1.rearrange("(p t) d a b -> p t (d a b)", t=16)
    x3_dram = x3.rearrange("(c p j) d -> c p j d", p=P, j=4)
    x2_dram = x2.flatten_outer_dims().rearrange("(h p s) d -> h p s d", p=P, s=2)
    w_dram = w.rearrange("(c p j) m -> p c j m", p=P, j=4)
    y_dram = x2.flatten_outer_dims()[PAIR_ROW:PAIR_ROW + 512, :].rearrange("(p s) d -> p s d", s=4)
    out_dram = out.rearrange("(p t) j -> p t j", t=16)

    with ExitStack() as ctx:
        const = ctx.enter_context(tc.tile_pool(name="const", bufs=1))
        keep = ctx.enter_context(tc.tile_pool(name="keep", bufs=1))
        stream = ctx.enter_context(tc.tile_pool(name="stream", bufs=2))
        psum = ctx.enter_context(tc.psum_pool(name="psum", bufs=1))
        ctx.enter_context(tc.manual_schedule())

        items = load_order()
        held = {"W": 0, "X": 0, "Q": 0, "Z": 0}
        raw = {}
        state = {"pos": 0}

        def load_ahead():
            while state["pos"] < len(items):
                kind, i = items[state["pos"]]
                if kind == "Y":
                    if held["X"] >= DEPTH["X"]:
                        break
                    t = stream.tile([P, 4, D], BF16, name="x2pair", tag="x3raw", bufs=DEPTH["X"])
                    for n in range(3):
                        nc.sync.dma_start(out=t[:, :, 512 * n:512 * n + 512], in_=y_dram[:, :, 512 * n:512 * n + 512])
                    raw[(kind, i)] = t
                    state["pos"] += 1
                    continue
                if held[kind] >= DEPTH[kind]:
                    break
                if kind == "W":
                    t = keep.tile([P, 8, 4, C], BF16, name="w_sb", tag="big0")
                    nc.sync.dma_start(out=t, in_=w_dram)
                elif kind == "X":
                    t = stream.tile([P, 4, D], BF16, name="x3raw", tag="x3raw", bufs=DEPTH["X"])
                    nc.sync.dma_start(out=t, in_=x3_dram[i])
                elif kind == "Z":
                    t = stream.tile([P, 2, D], BF16, name="x2raw", tag="x2raw", bufs=DEPTH["Z"])
                    nc.sync.dma_start(out=t, in_=x2_dram[i])
                else:
                    t = stream.tile([P, 2 * D], BF16, name="qraw", tag="qraw", bufs=DEPTH["Q"])
                    nc.sync.dma_start(out=t.rearrange("p (t d) -> p t d", t=2), in_=q_dram[:, 2 * i:2 * i + 2, :])
                raw[(kind, i)] = t
                held[kind] += 1
                state["pos"] += 1

        def release(kind):
            held[kind] -= 1
            load_ahead()

        load_ahead()

        ident = const.tile([P, P], F32, name="ident")
        make_identity(nc, ident)
        sel_f = const.tile([P, 16], F32, name="sel_f")
        nc.vector.tensor_reduce(out=sel_f, in_=ident.rearrange("p (n i) -> p n i", i=8), axis=AX.X, op=ALU.add)
        sel = const.tile([P, 16], BF16, name="sel")
        nc.vector.tensor_copy(out=sel, in_=sel_f)
        sel4_f = const.tile([P, 32], F32, name="sel4_f")
        nc.vector.tensor_reduce(out=sel4_f, in_=ident.rearrange("p (n i) -> p n i", i=4), axis=AX.X, op=ALU.add)
        sel4 = const.tile([P, 32], BF16, name="sel4")
        nc.vector.tensor_copy(out=sel4, in_=sel4_f)
        ones = const.tile([P, 2], BF16, name="ones")
        nc.vector.memset(ones, 1.0)

        q_codes = keep.tile([P, 8, 3 * 256], U32, name="q_codes", align_bytes=64)
        q_scales = keep.tile([P, 8, 3 * 256], U8, name="q_scales", align_bytes=64)
        q2 = keep.tile([P, 16], F32, name="q2")
        junk = keep.tile([P, D], BF16, name="junk")
        o_sb = keep.tile([P, 16, C], F32, name="o_sb")
        w_codes = keep.tile([P, 8 * C], U32, name="w_codes", align_bytes=64)
        w_scales = keep.tile([P, 8 * C], U8, name="w_scales", align_bytes=64)
        T = {}

        w_sb = raw[("W", 0)]
        w_g = keep.tile([P, 8, C, 4], BF16, name="w_g", tag="big1", align_bytes=64)
        nc.vector.tensor_copy(out=w_g[:, 0:4], in_=w_sb[:, 0:4].rearrange("p c j m -> p c m j"))
        nc.scalar.copy(out=w_g[:, 4:8], in_=w_sb[:, 4:8].rearrange("p c j m -> p c m j"))
        for h in range(2):
            nc.vector.quantize_mx(out=w_codes[:, 512 * h:512 * h + 512].bitcast(FP8X4),
                                  scales=w_scales[:, 512 * h:512 * h + 512],
                                  in_=w_g[:, 4 * h:4 * h + 4].rearrange("p c m j -> p (c m j)"))
        den_ps = psum.tile([P, 512], F32, name="den_ps", tag="zp", bufs=2)
        for c in range(8):
            for j in range(4):
                nc.tensor.matmul(out=den_ps[:, 0:2], lhsT=w_sb[:, c, j, :], rhs=ones,
                                 start=(c == 0 and j == 0), stop=(c == 7 and j == 3))
        den = const.tile([P, 1], F32, name="den")
        nc.vector.tensor_scalar(out=den, in0=den_ps[:, 0:1], scalar1=float(SHOT), scalar2=0.5, op0=ALU.add, op1=ALU.mult)
        rden = const.tile([P, 1], F32, name="rden")
        nc.vector.reciprocal(out=rden, in_=den)

        def regroup(copy, dst, src, lo, hi):
            copy(out=dst[:, lo:hi, :].rearrange("p (c i) t -> p c t i", i=4),
                 in_=src[:, :, lo:hi].rearrange("p t (c i) -> p c t i", i=4))

        def x_regroup(c):
            g = stream.tile([P, D, 4], BF16, name="x3g", tag="x3g", bufs=2, align_bytes=64)
            T[("g", c)] = g
            regroup(nc.vector.tensor_copy, g, raw[("X", c)], 0, D - S_COLS)
            regroup(nc.scalar.copy, g, raw[("X", c)], D - S_COLS, D)
            release("X")

        def x_quantise(c):
            codes = stream.tile([P, D], U32, name="x3c", tag="x3c", bufs=2, align_bytes=64)
            scales = stream.tile([P, D], U8, name="x3s", tag="x3s", bufs=2, align_bytes=64)
            T[("c", c)] = codes
            T[("s", c)] = scales
            for cols in (slice(0, 1024), slice(1024, 1536)):
                nc.vector.quantize_mx(out=codes[:, cols].bitcast(FP8X4), scales=scales[:, cols],
                                      in_=T[("g", c)][:, cols, :].rearrange("p c t -> p (c t)"))

        def x_matmul(c):
            for n in range(3):
                if c == 0:
                    T[("wu", n)] = psum.tile([P, 512], F32, name="wu%d" % n, tag="a%d" % n)
                cols = slice(512 * n, 512 * n + 512)
                nc.tensor.matmul_mx(out=T[("wu", n)], lhsT=w_codes[:, C * c:C * c + C].bitcast(FP8X4),
                                    lhsT_scale=w_scales[:, C * c:C * c + C],
                                    rhs=T[("c", c)][:, cols].bitcast(FP8X4), rhs_scale=T[("s", c)][:, cols],
                                    start=(c == 0), stop=(c == 7))

        def q_squares(k):
            for tt in range(2):
                nc.scalar.activation(out=junk, in_=raw[("Q", k)][:, D * tt:D * tt + D], func=ACT.Square,
                                     accum_out=q2[:, 2 * k + tt:2 * k + tt + 1])

        def q_transpose(k):
            words = raw[("Q", k)].bitcast(F32)
            for g in range(3):
                xt = psum.tile([P, 2, 2, P], F32, name="xt", tag="xt", bufs=3)
                T[("xt", k, g)] = xt
                for tt in range(2):
                    for u in range(2):
                        lo = 768 * tt + 256 * g + 128 * u
                        nc.tensor.transpose(out=xt[:, tt, u, :], in_=words[:, lo:lo + 128], identity=ident)

        def q_copy_out(k):
            qg = stream.tile([P, 3 * 256 * 4], BF16, name="qg", tag="qg", bufs=2, align_bytes=64)
            T[("qg", k)] = qg
            qg_w = qg.bitcast(F32)
            for g in range(3):
                nc.scalar.copy(out=qg_w[:, 512 * g:512 * g + 512].rearrange("p (t i u) -> p t i u", t=2, u=2),
                               in_=T[("xt", k, g)].rearrange("p t u i -> p t i u"))

        def q_quantise(k):
            for cols in (slice(0, 512), slice(512, 768)):
                nc.vector.quantize_mx(out=q_codes[:, k, cols].bitcast(FP8X4), scales=q_scales[:, k, cols],
                                      in_=T[("qg", k)][:, 4 * cols.start:4 * cols.stop])

        def z_sum(h):
            zp = psum.tile([P, 512], F32, name="zp", tag="zp", bufs=2)
            zv = zp[:, 0:192].rearrange("p (t n) -> p t n", n=16)
            T[("zv", h)] = zv
            for dt in range(12):
                for s in range(2):
                    nc.tensor.matmul(out=zv[:, dt, :], lhsT=raw[("Z", h)][:, s, P * dt:P * dt + P], rhs=sel,
                                     start=(s == 0), stop=(s == 1))
            release("Z")

        def z_copy_out(h):
            if "st_sb" not in T:
                T["st_sb"] = keep.tile([P, 12, C], F32, name="st_sb", tag="big0")
            nc.scalar.copy(out=T["st_sb"][:, :, 16 * h:16 * h + 16], in_=T[("zv", h)])

        def pair_sum(n):
            zp = psum.tile([P, 512], F32, name="zq", tag="xt", bufs=3)
            zv = zp[:, 0:128].rearrange("p (t n) -> p t n", n=32)
            T[("yv", n)] = zv
            for dt in range(4 * n, 4 * n + 4):
                for s in range(4):
                    nc.tensor.matmul(out=zv[:, dt - 4 * n, :], lhsT=raw[("Y", 0)][:, s, P * dt:P * dt + P], rhs=sel4,
                                     start=(s == 0), stop=(s == 3))

        def pair_copy_out(n):
            nc.scalar.copy(out=T["st_sb"][:, 4 * n:4 * n + 4, 96:128], in_=T[("yv", n)])

        def wu_scaled(n):
            if "wusc" not in T:
                T["wusc"] = keep.tile([P, D], F32, name="wusc", tag="big1", align_bytes=64)
            nc.scalar.activation(out=T["wusc"][:, 512 * n:512 * n + 512], in_=T[("wu", n)], func=ACT.Copy,
                                 scale=rden[:, 0:1])

        for r in range(ROUNDS + 1):
            if r < ROUNDS:
                x_regroup(r)
                q_squares(r)
                q_transpose(r)
                release("Q")
                q_copy_out(r)
            if r >= 1:
                q_quantise(r - 1)
            if r < ROUNDS:
                x_quantise(r)
            for h in Z_OF_ROUND.get(r, []):
                z_sum(h)
                z_copy_out(h)
            if r == ROUNDS:
                pair_sum(0)
                pair_copy_out(0)
            if r >= 1:
                x_matmul(r - 1)

        wu_scaled(0)
        wu_scaled(1)
        pair_sum(1)
        pair_copy_out(1)
        wu_scaled(2)

        s_ps = []

        def s_back(b):
            t = psum.tile([P, 512], F32, name="s_ps%d" % b, tag="a%d" % b)
            s_ps.append(t)
            for i in range(4):
                nc.tensor.transpose(out=t[:, P * i:P * i + P], in_=T["st_sb"][:, 4 * b + i, :], identity=ident)

        s_back(0)
        pair_sum(2)
        pair_copy_out(2)
        s_back(1)
        s_back(2)
        proto = keep.tile([P, 3, 2, 2 * P], F32, name="proto")
        for b in range(3):
            nc.vector.scalar_tensor_tensor(
                out=proto[:, b].rearrange("j e v -> j v e"),
                in0=s_ps[b].rearrange("j (v e) -> j v e", e=2), scalar=rden[:, 0:1],
                in1=T["wusc"][:, 512 * b:512 * b + 512].rearrange("j (v e) -> j v e", e=2),
                op0=ALU.mult, op1=ALU.add)
        pt = []
        for g in range(3):
            t = psum.tile([P, 4, C], F32, name="pt%d" % g, tag="a%d" % g)
            pt.append(t)
            for u in range(2):
                for e in range(2):
                    nc.tensor.transpose(out=t[:, 2 * u + e, :], in_=proto[:, g, e, P * u:P * u + P], identity=ident)
        p2parts = const.tile([P, 3], F32, name="p2parts")
        p2sums = const.tile([P, 2], F32, name="p2sums")
        for b in range(3):
            nc.scalar.activation(out=junk[:, 0:512], in_=proto[:, b].rearrange("j e v -> j (e v)"), func=ACT.Square,
                                 scale=0.5, accum_out=p2parts[:, b:b + 1])
            if b >= 1:
                nc.scalar.activation(out=p2sums[:, b - 1:b], in_=p2parts[:, b:b + 1], func=ACT.Identity,
                                     bias=(p2parts[:, 0:1] if b == 1 else p2sums[:, 0:1]), scale=1.0)
        pg = keep.tile([P, 3, C, 4], BF16, name="pg", align_bytes=64)
        p_codes = keep.tile([P, 3, C], U32, name="p_codes", align_bytes=64)
        p_scales = keep.tile([P, 3, C], U8, name="p_scales", align_bytes=64)

        def p_copy_out(copy, g):
            copy(out=pg[:, g], in_=pt[g].rearrange("p t j -> p j t"))

        def p_quantise(g):
            nc.vector.quantize_mx(out=p_codes[:, g, :].bitcast(FP8X4), scales=p_scales[:, g, :],
                                  in_=pg[:, g].rearrange("p j t -> p (j t)"))

        def cross_pass(dst, t, g):
            cols = slice(256 * g + P * (t % 2), 256 * g + P * (t % 2) + P)
            nc.tensor.matmul_mx(out=dst, lhsT=q_codes[:, t // 2, cols].bitcast(FP8X4), lhsT_scale=q_scales[:, t // 2, cols],
                                rhs=p_codes[:, g, :].bitcast(FP8X4), rhs_scale=p_scales[:, g, :],
                                start=(g == 0), stop=(g == 2))

        def finish(src, t):
            nc.vector.scalar_tensor_tensor(out=o_sb[:, t, :], in0=src, scalar=q2[:, t:t + 1], in1=p2b,
                                           op0=ALU.subtract, op1=ALU.subtract)
            for first, last in STORES:
                if last == t:
                    nc.sync.dma_start(out=out_dram[:, first:last + 1, :], in_=o_sb[:, first:last + 1, :])

        first_banks = []
        for t in range(FIRST):
            bank = psum.tile([P, 512], F32, name="cr", tag=FIRST_TAGS[t], bufs=TAG_BUFS[FIRST_TAGS[t]])
            first_banks.append(bank)
        p_copy_out(nc.vector.tensor_copy, 0)
        p_quantise(0)
        p2b_ps = psum.tile([P, 512], F32, name="p2b_ps", tag="a0")
        nc.tensor.matmul(out=p2b_ps[:, 0:C], lhsT=p2sums[:, 1:2].to_broadcast([P, P]), rhs=ident, start=True, stop=True)
        for t in range(FIRST):
            cross_pass(first_banks[t][:, 0:C], t, 0)
        p_copy_out(nc.vector.tensor_copy, 2)
        p_copy_out(nc.scalar.copy, 1)
        p2b = keep.tile([P, C], F32, name="p2b")
        nc.scalar.copy(out=p2b, in_=p2b_ps[:, 0:C])
        p_quantise(1)
        for t in range(FIRST):
            cross_pass(first_banks[t][:, 0:C], t, 1)
        p_quantise(2)
        for t in range(FIRST):
            cross_pass(first_banks[t][:, 0:C], t, 2)

        for t in range(FIRST):
            finish(first_banks[t][:, 0:C], t)
        for n, t0 in enumerate(range(FIRST, 16, 2)):
            tag = LATER_TAGS[n]
            bank = psum.tile([P, 512], F32, name="cr", tag=tag, bufs=TAG_BUFS[tag])
            pair = [t for t in (t0, t0 + 1) if t < 16]
            for i, t in enumerate(pair):
                for g in range(3):
                    cross_pass(bank[:, C * i:C * i + C], t, g)
            for i, t in enumerate(pair):
                finish(bank[:, C * i:C * i + C], t)
